import numpy as np
import ml_dtypes


def mxq(x, axis, fmt="e4m3"):
    dtype, down = {"e4m3": (ml_dtypes.float8_e4m3fn, 7), "e5m2": (ml_dtypes.float8_e5m2, 14)}[fmt]
    v = np.moveaxis(np.asarray(x, np.float32).astype(ml_dtypes.bfloat16).astype(np.float64), axis, -1)
    blocks = v.reshape(v.shape[:-1] + (-1, 32))
    amax = np.abs(blocks).max(-1, keepdims=True)
    byte = np.maximum(np.where(amax > 0, np.frexp(amax)[1] - 1 + 127, 0) - down, 1)
    scale = np.exp2(byte - 127.0)
    codes = (blocks / scale).astype(np.float32).astype(dtype).astype(np.float64)
    return np.moveaxis((codes * scale).reshape(v.shape), -1, axis)


WIDE = False


def mx_kscale(k):
    if not WIDE:
        return np.ones(k)
    levels = np.array([10, -10, 5, -5, 0])
    a = np.random.permutation(np.resize(levels, k // 512 * 4)).reshape(k // 512, 4)
    idx = np.arange(k)
    return np.exp2(a[idx // 512, idx % 128 // 32])


BF16 = ml_dtypes.bfloat16


def bf(x):
    return np.asarray(x, np.float32).astype(BF16)


def f64(x):
    return np.asarray(x).astype(np.float64)


B, T, D, DV = 8, 1024, 128, 256


def sigmoid(u):
    return 1.0 / (1.0 + np.exp(-u))


def setup_inputs():
    s = mx_kscale(T)
    q = np.random.standard_normal((B, T, D)) * 1.6
    k = np.random.standard_normal((B, T, D)) * 1.6
    q[..., 0] = 4.0
    q[..., 1] = -4.0
    k[..., 0] += np.log(s)[None, :] * np.sqrt(D) / 4.0
    v = np.random.standard_normal((B, T, DV)) * s[None, :, None] * np.mean(1.0 / s)
    return {"q": bf(q),
            "k": bf(k),
            "v": bf(v),
            "mask": (np.random.random((1, T, T)) < 0.7).astype(np.int32),
            "mode": bf(0.5 + 0.3 * np.random.standard_normal(1))}


def reference(q, k, v, mask, mode):
    q, k, v = f64(q), f64(k), f64(v)
    scale = D ** (-0.5)
    meson = -(q @ k.transpose(0, 2, 1)) * scale
    k_perm = np.roll(k, 1, axis=-1)
    baryon = (q @ k_perm.transpose(0, 2, 1)) * scale
    alpha = sigmoid(f64(mode))
    attn = alpha * meson + (1.0 - alpha) * baryon
    attn = np.where(f64(mask) == 0.0, -np.inf, attn)
    e = np.exp(attn - attn.max(-1, keepdims=True))
    return (mxq(e, 2, "e4m3") @ mxq(v, 1, "e4m3")) / e.sum(-1, keepdims=True)

@@ -1,0 +1,190 @@
+from contextlib import ExitStack
+
+import concourse.mybir as mybir
+from concourse.masks import make_identity
+
+F32 = mybir.dt.float32
+BF16 = mybir.dt.bfloat16
+I32 = mybir.dt.int32
+U32 = mybir.dt.uint32
+U8 = mybir.dt.uint8
+FP8X4 = mybir.dt.float8_e4m3fn_x4
+ALU = mybir.AluOpType
+ACT = mybir.ActivationFunctionType
+AX = mybir.AxisListType
+
+B, T, D, DV = 8, 1024, 128, 256
+P = 128
+TILES = T // P
+BANK = 512
+HALVES = T // BANK
+PACK = 4
+K_PASS = P * PACK
+PASSES = T // K_PASS
+MASKED = -(2.0**100)
+
+FLOPS = 2 * (2 * B * T * T * D) + 2 * B * T * T * DV
+
+
+def tile_dualmodehead_t_kernel(tc, q, k, v, mask, mode, out):
+    nc = tc.nc
+    mask_words = mask.bitcast(I32).rearrange("o q w -> (o q) w")
+    words = mask_words.shape[1] // T
+
+    with ExitStack() as ctx:
+        const = ctx.enter_context(tc.tile_pool(name="const", bufs=1))
+        loads = ctx.enter_context(tc.tile_pool(name="loads", bufs=2))
+        blend = ctx.enter_context(tc.tile_pool(name="blend", bufs=2))
+        batch = ctx.enter_context(tc.tile_pool(name="batch", bufs=2))
+        work = ctx.enter_context(tc.tile_pool(name="work", bufs=3))
+        small = ctx.enter_context(tc.tile_pool(name="small", bufs=4))
+        psum_s = ctx.enter_context(tc.psum_pool(name="psum_s", bufs=4))
+        psum_e = ctx.enter_context(tc.psum_pool(name="psum_e", bufs=2))
+        psum_o = ctx.enter_context(tc.psum_pool(name="psum_o", bufs=1))
+        psum_t = ctx.enter_context(tc.psum_pool(name="psum_t", bufs=1))
+
+        ident_bf = const.tile([P, P], BF16)
+        make_identity(nc, ident_bf[:])
+        ident_f32 = const.tile([P, P], F32)
+        make_identity(nc, ident_f32[:])
+
+        mode_bc = const.tile([P, 1], BF16)
+        nc.sync.dma_start(out=mode_bc[:], in_=mode.partition_broadcast(P))
+        exp_neg = const.tile([P, 1], F32)
+        nc.scalar.activation(out=exp_neg[:], in_=mode_bc[:], func=ACT.Exp, scale=-1.0)
+        denom = const.tile([P, 1], F32)
+        nc.vector.tensor_scalar_add(out=denom[:], in0=exp_neg[:], scalar1=1.0)
+        alpha = const.tile([P, 1], F32)
+        nc.vector.reciprocal(out=alpha[:], in_=denom[:])
+        c_meson = const.tile([P, 1], F32)
+        nc.vector.tensor_scalar_mul(out=c_meson[:], in0=alpha[:], scalar1=-(D**-0.5))
+        c_baryon = const.tile([P, 1], F32)
+        nc.vector.tensor_scalar_add(out=c_baryon[:], in0=c_meson[:], scalar1=D**-0.5)
+
+        mask_bias = const.tile([P, TILES, T], BF16)
+
+        def load_mask_bias(i):
+            mask_raw = loads.tile([P, T, words], I32)
+            nc.sync.dma_start(
+                out=mask_raw[:].rearrange("p k w -> p (k w)"), in_=mask_words[i * P : (i + 1) * P, :]
+            )
+            nc.vector.tensor_scalar(
+                out=mask_bias[:, i, :],
+                in0=mask_raw[:, :, 0],
+                scalar1=-MASKED,
+                scalar2=MASKED,
+                op0=ALU.mult,
+                op1=ALU.add,
+            )
+
+        def transpose_tokens(natural, name):
+            bank = psum_t.tile([P, T], BF16, name="bank_t")
+            for j in range(TILES):
+                nc.tensor.transpose(bank[:, j * P : (j + 1) * P], natural[:, j, :], ident_bf[:])
+            turned = batch.tile([P, T], BF16, name=name)
+            nc.scalar.copy(out=turned[:], in_=bank[:])
+            return turned
+
+        for b in range(B):
+            k_nat = loads.tile([P, TILES, D], BF16)
+            nc.sync.dma_start(out=k_nat[:], in_=k[b].rearrange("(j p) d -> p j d", p=P))
+            q_nat = loads.tile([P, TILES, D], BF16)
+            nc.sync.dma_start(out=q_nat[:], in_=q[b].rearrange("(j p) d -> p j d", p=P))
+            v_raw = loads.tile([P, PASSES, PACK, DV], BF16)
+            nc.sync.dma_start(
+                out=v_raw[:].rearrange("p g (u e) w -> p (g u) (e w)", e=2),
+                in_=v[b].rearrange("(c p e) w -> p c (e w)", p=P, e=2),
+            )
+
+            k_meson = blend.tile([P, TILES, D], F32)
+            nc.gpsimd.tensor_scalar(
+                out=k_meson[:], in0=k_nat[:], scalar1=c_meson[:, 0:1], scalar2=0.0,
+                op0=ALU.mult, op1=ALU.add,
+            )
+            k_baryon = blend.tile([P, TILES, D], F32)
+            nc.gpsimd.tensor_scalar(
+                out=k_baryon[:, :, 1:D], in0=k_nat[:, :, 0 : D - 1], scalar1=c_baryon[:, 0:1],
+                scalar2=0.0, op0=ALU.mult, op1=ALU.add,
+            )
+            nc.gpsimd.tensor_scalar(
+                out=k_baryon[:, :, 0:1], in0=k_nat[:, :, D - 1 : D], scalar1=c_baryon[:, 0:1],
+                scalar2=0.0, op0=ALU.mult, op1=ALU.add,
+            )
+            k_blend = blend.tile([P, TILES, D], F32)
+            nc.gpsimd.tensor_tensor(out=k_blend[:], in0=k_meson[:], in1=k_baryon[:], op=ALU.add)
+            k_hi = blend.tile([P, TILES, D], BF16)
+            nc.gpsimd.tensor_scalar(
+                out=k_hi[:], in0=k_blend[:], scalar1=1.0, scalar2=0.0, op0=ALU.mult, op1=ALU.add
+            )
+            k_lo = blend.tile([P, TILES, D], BF16)
+            nc.gpsimd.tensor_tensor(out=k_lo[:], in0=k_blend[:], in1=k_hi[:], op=ALU.subtract)
+
+            qT = transpose_tokens(q_nat, "qT")
+            hiT = transpose_tokens(k_hi, "hiT")
+            loT = transpose_tokens(k_lo, "loT")
+
+            v_grouped = batch.tile([P, PASSES, DV, PACK], BF16, align_bytes=64)
+            nc.gpsimd.tensor_scalar(
+                out=v_grouped[:], in0=v_raw[:].rearrange("p g t w -> p g w t"), scalar1=1.0,
+                scalar2=0.0, op0=ALU.mult, op1=ALU.add,
+            )
+            v_codes = batch.tile([P, PASSES * DV], U32, align_bytes=64)
+            v_scales = batch.tile([P, PASSES * DV], U8, align_bytes=64)
+            nc.vector.quantize_mx(
+                out=v_codes[:].bitcast(FP8X4),
+                scales=v_scales[:],
+                in_=v_grouped[:].rearrange("p g w t -> p (g w t)"),
+            )
+
+            for i in range(TILES):
+                if b == 0:
+                    load_mask_bias(i)
+                queries = slice(i * P, (i + 1) * P)
+
+                s_masked = work.tile([P, T], F32)
+                for h in range(HALVES):
+                    keys = slice(h * BANK, (h + 1) * BANK)
+                    s_bank = psum_s.tile([P, BANK], F32)
+                    nc.tensor.matmul(s_bank[:], lhsT=qT[:, queries], rhs=hiT[:, keys], start=True, stop=False)
+                    nc.tensor.matmul(s_bank[:], lhsT=qT[:, queries], rhs=loT[:, keys], start=False, stop=True)
+                    nc.vector.tensor_tensor(
+                        out=s_masked[:, keys], in0=s_bank[:], in1=mask_bias[:, i, keys], op=ALU.add
+                    )
+                neg_max = small.tile([P, 1], F32)
+                nc.vector.tensor_reduce(out=neg_max[:], in_=s_masked[:], axis=AX.X, op=ALU.max, negate=True)
+                e = work.tile([P, T], BF16)
+                row_sum = small.tile([P, 1], F32)
+                nc.scalar.activation(
+                    out=e[:], in_=s_masked[:], func=ACT.Exp, bias=neg_max[:, 0:1], scale=1.0,
+                    accum_out=row_sum[:],
+                )
+                inv_sum = small.tile([P, 1], F32)
+                nc.vector.reciprocal(out=inv_sum[:], in_=row_sum[:])
+
+                e_words = e[:].bitcast(F32)
+                eT_bank = psum_e.tile([P, PASSES * 2, P], F32)
+                for c in range(PASSES * 2):
+                    nc.tensor.transpose(eT_bank[:, c, :], e_words[:, c * P : (c + 1) * P], ident_f32[:])
+                e_grouped = work.tile([P, PASSES * P * PACK], BF16, align_bytes=64)
+                nc.scalar.copy(
+                    out=e_grouped[:].bitcast(F32).rearrange("p (g q u) -> p g q u", g=PASSES, u=2),
+                    in_=eT_bank[:].rearrange("p (g u) q -> p g q u", u=2),
+                )
+                e_codes = work.tile([P, PASSES * P], U32, align_bytes=64)
+                e_scales = work.tile([P, PASSES * P], U8, align_bytes=64)
+                nc.vector.quantize_mx(out=e_codes[:].bitcast(FP8X4), scales=e_scales[:], in_=e_grouped[:])
+
+                o_bank = psum_o.tile([P, DV], F32)
+                for g in range(PASSES):
+                    nc.tensor.matmul_mx(
+                        out=o_bank[:],
+                        lhsT=e_codes[:, g * P : (g + 1) * P].bitcast(FP8X4),
+                        lhsT_scale=e_scales[:, g * P : (g + 1) * P],
+                        rhs=v_codes[:, g * DV : (g + 1) * DV].bitcast(FP8X4),
+                        rhs_scale=v_scales[:, g * DV : (g + 1) * DV],
+                        start=(g == 0),
+                        stop=(g == PASSES - 1),
+                    )
+                o_sb = work.tile([P, DV], F32)
+                nc.scalar.activation(out=o_sb[:], in_=o_bank[:], func=ACT.Copy, scale=inv_sum[:, 0:1])
+                nc.sync.dma_start(out=out[b, queries, :], in_=o_sb[:])

@@ -61,21 +61,30 @@ def tile_dualmodehead_t_kernel(tc, q, k, v, mask, mode, out):
         c_baryon = const.tile([P, 1], F32)
         nc.vector.tensor_scalar_add(out=c_baryon[:], in0=c_meson[:], scalar1=D**-0.5)
 
-        mask_bias = const.tile([P, TILES, T], BF16)
+        mask_biasT = const.tile([P, TILES, TILES, P], F32)
 
         def load_mask_bias(i):
             mask_raw = loads.tile([P, T, words], I32)
             nc.sync.dma_start(
                 out=mask_raw[:].rearrange("p k w -> p (k w)"), in_=mask_words[i * P : (i + 1) * P, :]
             )
+            bias_rows = work.tile([P, T], F32)
             nc.vector.tensor_scalar(
-                out=mask_bias[:, i, :],
+                out=bias_rows[:],
                 in0=mask_raw[:, :, 0],
                 scalar1=-MASKED,
                 scalar2=MASKED,
                 op0=ALU.mult,
                 op1=ALU.add,
             )
+            for h in range(HALVES):
+                bank = psum_t.tile([P, BANK // P, P], F32, name="bank_m", tag="bank_t")
+                for r in range(BANK // P):
+                    j = h * (BANK // P) + r
+                    nc.tensor.transpose(bank[:, r, :], bias_rows[:, j * P : (j + 1) * P], ident_f32[:])
+                nc.vector.tensor_copy(
+                    out=mask_biasT[:, i, h * (BANK // P) : (h + 1) * (BANK // P), :], in_=bank[:]
+                )
 
         def transpose_tokens(natural, name):
             bank = psum_t.tile([P, T], BF16, name="bank_t")
@@ -141,23 +150,35 @@ def tile_dualmodehead_t_kernel(tc, q, k, v, mask, mode, out):
                     load_mask_bias(i)
                 queries = slice(i * P, (i + 1) * P)
 
-                s_masked = work.tile([P, T], F32)
+                s_banks = []
+                bank_max = small.tile([P, HALVES], F32)
                 for h in range(HALVES):
                     keys = slice(h * BANK, (h + 1) * BANK)
                     s_bank = psum_s.tile([P, BANK], F32)
+                    s_banks.append(s_bank)
                     nc.tensor.matmul(s_bank[:], lhsT=qT[:, queries], rhs=hiT[:, keys], start=True, stop=False)
-                    nc.tensor.matmul(s_bank[:], lhsT=qT[:, queries], rhs=loT[:, keys], start=False, stop=True)
-                    nc.vector.tensor_tensor(
-                        out=s_masked[:, keys], in0=s_bank[:], in1=mask_bias[:, i, keys], op=ALU.add
-                    )
+                    nc.tensor.matmul(s_bank[:], lhsT=qT[:, queries], rhs=loT[:, keys], start=False, stop=False)
+                    for r in range(BANK // P):
+                        nc.tensor.matmul(
+                            s_bank[:, r * P : (r + 1) * P],
+                            lhsT=mask_biasT[:, i, h * (BANK // P) + r, :],
+                            rhs=ident_f32[:],
+                            is_transpose=True,
+                            start=False,
+                            stop=(r == BANK // P - 1),
+                        )
+                    nc.vector.tensor_reduce(out=bank_max[:, h : h + 1], in_=s_bank[:], axis=AX.X, op=ALU.max)
                 neg_max = small.tile([P, 1], F32)
-                nc.vector.tensor_reduce(out=neg_max[:], in_=s_masked[:], axis=AX.X, op=ALU.max, negate=True)
+                nc.vector.tensor_reduce(out=neg_max[:], in_=bank_max[:], axis=AX.X, op=ALU.max, negate=True)
                 e = work.tile([P, T], BF16)
+                bank_sum = small.tile([P, HALVES], F32)
+                for h in range(HALVES):
+                    nc.scalar.activation(
+                        out=e[:, h * BANK : (h + 1) * BANK], in_=s_banks[h][:], func=ACT.Exp,
+                        bias=neg_max[:, 0:1], scale=1.0, accum_out=bank_sum[:, h : h + 1],
+                    )
                 row_sum = small.tile([P, 1], F32)
-                nc.scalar.activation(
-                    out=e[:], in_=s_masked[:], func=ACT.Exp, bias=neg_max[:, 0:1], scale=1.0,
-                    accum_out=row_sum[:],
-                )
+                nc.vector.tensor_reduce(out=row_sum[:], in_=bank_sum[:], axis=AX.X, op=ALU.add)
                 inv_sum = small.tile([P, 1], F32)
                 nc.vector.reciprocal(out=inv_sum[:], in_=row_sum[:])
 

@@ -16,11 +16,15 @@ AX = mybir.AxisListType
 B, T, D, DV = 8, 1024, 128, 256
 P = 128
 TILES = T // P
+N_TILES = B * TILES
 BANK = 512
 HALVES = T // BANK
+BLOCKS = BANK // P
 PACK = 4
 K_PASS = P * PACK
 PASSES = T // K_PASS
+GROUP = 2
+MASK_WORDS = 2
 MASKED = -(2.0**100)
 
 FLOPS = 2 * (2 * B * T * T * D) + 2 * B * T * T * DV
@@ -28,20 +32,20 @@ FLOPS = 2 * (2 * B * T * T * D) + 2 * B * T * T * DV
 
 def tile_dualmodehead_t_kernel(tc, q, k, v, mask, mode, out):
     nc = tc.nc
-    mask_words = mask.bitcast(I32).rearrange("o q w -> (o q) w")
-    words = mask_words.shape[1] // T
+    mask_rows = mask.bitcast(I32).rearrange("o q w -> (o q) w")
+    assert mask_rows.shape[1] == T * MASK_WORDS
 
     with ExitStack() as ctx:
         const = ctx.enter_context(tc.tile_pool(name="const", bufs=1))
         loads = ctx.enter_context(tc.tile_pool(name="loads", bufs=2))
-        blend = ctx.enter_context(tc.tile_pool(name="blend", bufs=2))
         batch = ctx.enter_context(tc.tile_pool(name="batch", bufs=2))
         work = ctx.enter_context(tc.tile_pool(name="work", bufs=3))
-        small = ctx.enter_context(tc.tile_pool(name="small", bufs=4))
+        small = ctx.enter_context(tc.tile_pool(name="small", bufs=6))
         psum_s = ctx.enter_context(tc.psum_pool(name="psum_s", bufs=4))
         psum_e = ctx.enter_context(tc.psum_pool(name="psum_e", bufs=2))
         psum_o = ctx.enter_context(tc.psum_pool(name="psum_o", bufs=1))
         psum_t = ctx.enter_context(tc.psum_pool(name="psum_t", bufs=1))
+        ctx.enter_context(tc.manual_schedule())
 
         ident_bf = const.tile([P, P], BF16)
         make_identity(nc, ident_bf[:])
@@ -61,151 +65,260 @@ def tile_dualmodehead_t_kernel(tc, q, k, v, mask, mode, out):
         c_baryon = const.tile([P, 1], F32)
         nc.vector.tensor_scalar_add(out=c_baryon[:], in0=c_meson[:], scalar1=D**-0.5)
 
-        mask_biasT = const.tile([P, TILES, TILES, P], F32)
+        mask_bias = const.tile([P, TILES, T], BF16)
 
-        def load_mask_bias(i):
-            mask_raw = loads.tile([P, T, words], I32)
+        mask_raw = {}
+
+        def load_mask(i):
+            mask_raw[i] = loads.tile([P, T, MASK_WORDS], I32, name="mask_raw")
             nc.sync.dma_start(
-                out=mask_raw[:].rearrange("p k w -> p (k w)"), in_=mask_words[i * P : (i + 1) * P, :]
+                out=mask_raw[i][:].rearrange("p k w -> p (k w)"), in_=mask_rows[i * P : (i + 1) * P, :]
             )
-            bias_rows = work.tile([P, T], F32)
-            nc.vector.tensor_scalar(
-                out=bias_rows[:],
-                in0=mask_raw[:, :, 0],
-                scalar1=-MASKED,
-                scalar2=MASKED,
-                op0=ALU.mult,
-                op1=ALU.add,
+
+        def convert_mask(i):
+            nc.scalar.activation(
+                out=mask_bias[:, i, :], in_=mask_raw[i][:].bitcast(U32)[:, :, 0], func=ACT.Copy,
+                scale=-MASKED, bias=MASKED,
             )
-            for h in range(HALVES):
-                bank = psum_t.tile([P, BANK // P, P], F32, name="bank_m", tag="bank_t")
-                for r in range(BANK // P):
-                    j = h * (BANK // P) + r
-                    nc.tensor.transpose(bank[:, r, :], bias_rows[:, j * P : (j + 1) * P], ident_f32[:])
-                nc.vector.tensor_copy(
-                    out=mask_biasT[:, i, h * (BANK // P) : (h + 1) * (BANK // P), :], in_=bank[:]
-                )
 
-        def transpose_tokens(natural, name):
-            bank = psum_t.tile([P, T], BF16, name="bank_t")
-            for j in range(TILES):
-                nc.tensor.transpose(bank[:, j * P : (j + 1) * P], natural[:, j, :], ident_bf[:])
-            turned = batch.tile([P, T], BF16, name=name)
-            nc.scalar.copy(out=turned[:], in_=bank[:])
-            return turned
+        natural = {}
+        operand = {}
 
-        for b in range(B):
-            k_nat = loads.tile([P, TILES, D], BF16)
+        def load_batch(b):
+            k_nat = loads.tile([P, TILES, D], BF16, name="k_nat")
             nc.sync.dma_start(out=k_nat[:], in_=k[b].rearrange("(j p) d -> p j d", p=P))
-            q_nat = loads.tile([P, TILES, D], BF16)
+            q_nat = loads.tile([P, TILES, D], BF16, name="q_nat")
             nc.sync.dma_start(out=q_nat[:], in_=q[b].rearrange("(j p) d -> p j d", p=P))
-            v_raw = loads.tile([P, PASSES, PACK, DV], BF16)
+            natural[b] = {"k": k_nat, "q": q_nat}
+            operand[b] = {}
+
+        def load_values(b):
+            v_raw = loads.tile([P, PASSES, PACK, DV], BF16, name="v_raw")
             nc.sync.dma_start(
                 out=v_raw[:].rearrange("p g (u e) w -> p (g u) (e w)", e=2),
                 in_=v[b].rearrange("(c p e) w -> p c (e w)", p=P, e=2),
             )
+            natural[b]["v"] = v_raw
 
-            k_meson = blend.tile([P, TILES, D], F32)
-            nc.gpsimd.tensor_scalar(
-                out=k_meson[:], in0=k_nat[:], scalar1=c_meson[:, 0:1], scalar2=0.0,
-                op0=ALU.mult, op1=ALU.add,
-            )
-            k_baryon = blend.tile([P, TILES, D], F32)
-            nc.gpsimd.tensor_scalar(
-                out=k_baryon[:, :, 1:D], in0=k_nat[:, :, 0 : D - 1], scalar1=c_baryon[:, 0:1],
-                scalar2=0.0, op0=ALU.mult, op1=ALU.add,
-            )
-            nc.gpsimd.tensor_scalar(
-                out=k_baryon[:, :, 0:1], in0=k_nat[:, :, D - 1 : D], scalar1=c_baryon[:, 0:1],
-                scalar2=0.0, op0=ALU.mult, op1=ALU.add,
-            )
-            k_blend = blend.tile([P, TILES, D], F32)
-            nc.gpsimd.tensor_tensor(out=k_blend[:], in0=k_meson[:], in1=k_baryon[:], op=ALU.add)
-            k_hi = blend.tile([P, TILES, D], BF16)
-            nc.gpsimd.tensor_scalar(
-                out=k_hi[:], in0=k_blend[:], scalar1=1.0, scalar2=0.0, op0=ALU.mult, op1=ALU.add
-            )
-            k_lo = blend.tile([P, TILES, D], BF16)
-            nc.gpsimd.tensor_tensor(out=k_lo[:], in0=k_blend[:], in1=k_hi[:], op=ALU.subtract)
+        def blend_keys(b, engine):
+            k_nat = natural[b]["k"]
+            k_meson = loads.tile([P, TILES, D], F32, name="k_meson")
+            k_baryon = loads.tile([P, TILES, D], F32, name="k_baryon")
+            k_parts = loads.tile([P, 2, TILES, D], BF16, name="k_parts")
+            for h in range(HALVES):
+                js = slice(h * BLOCKS, (h + 1) * BLOCKS)
+                engine.tensor_scalar(
+                    out=k_meson[:, js, :], in0=k_nat[:, js, :], scalar1=c_meson[:, 0:1], scalar2=0.0,
+                    op0=ALU.mult, op1=ALU.add,
+                )
+                engine.tensor_scalar(
+                    out=k_baryon[:, js, 1:D], in0=k_nat[:, js, 0 : D - 1], scalar1=c_baryon[:, 0:1],
+                    scalar2=0.0, op0=ALU.mult, op1=ALU.add,
+                )
+                engine.tensor_scalar(
+                    out=k_baryon[:, js, 0:1], in0=k_nat[:, js, D - 1 : D], scalar1=c_baryon[:, 0:1],
+                    scalar2=0.0, op0=ALU.mult, op1=ALU.add,
+                )
+                engine.tensor_tensor(out=k_meson[:, js, :], in0=k_meson[:, js, :], in1=k_baryon[:, js, :], op=ALU.add)
+                engine.tensor_scalar(
+                    out=k_parts[:, 0, js, :], in0=k_meson[:, js, :], scalar1=1.0, scalar2=0.0,
+                    op0=ALU.mult, op1=ALU.add,
+                )
+                engine.tensor_tensor(
+                    out=k_parts[:, 1, js, :], in0=k_meson[:, js, :], in1=k_parts[:, 0, js, :], op=ALU.subtract
+                )
+            natural[b]["k_parts"] = k_parts
 
-            qT = transpose_tokens(q_nat, "qT")
-            hiT = transpose_tokens(k_hi, "hiT")
-            loT = transpose_tokens(k_lo, "loT")
+        def group_values(b, engine):
+            v_grouped = loads.tile([P, PASSES, DV, PACK], BF16, name="v_grouped", align_bytes=64)
+            for g in range(PASSES):
+                engine.tensor_scalar(
+                    out=v_grouped[:, g, :, :], in0=natural[b]["v"][:, g, :, :].rearrange("p t w -> p w t"),
+                    scalar1=1.0, scalar2=0.0, op0=ALU.mult, op1=ALU.add,
+                )
+            natural[b]["v_grouped"] = v_grouped
 
-            v_grouped = batch.tile([P, PASSES, DV, PACK], BF16, align_bytes=64)
-            nc.gpsimd.tensor_scalar(
-                out=v_grouped[:], in0=v_raw[:].rearrange("p g t w -> p g w t"), scalar1=1.0,
-                scalar2=0.0, op0=ALU.mult, op1=ALU.add,
+        def turn_queries(b):
+            bank = psum_t.tile([P, T], BF16, name="bank_q", tag="bank_t")
+            for j in range(TILES):
+                nc.tensor.transpose(bank[:, j * P : (j + 1) * P], natural[b]["q"][:, j, :], ident_bf[:])
+            qT = batch.tile([P, T], BF16, name="qT")
+            nc.scalar.copy(out=qT[:], in_=bank[:])
+            operand[b]["qT"] = qT
+
+        def turn_keys(b, h):
+            if h == 0:
+                operand[b]["kT"] = batch.tile([P, HALVES, 2, BANK], BF16, name="kT")
+            bank = psum_t.tile([P, 2, BLOCKS, P], BF16, name="bank_k", tag="bank_t")
+            for part in range(2):
+                for r in range(BLOCKS):
+                    nc.tensor.transpose(
+                        bank[:, part, r, :], natural[b]["k_parts"][:, part, h * BLOCKS + r, :], ident_bf[:]
+                    )
+            nc.scalar.copy(
+                out=operand[b]["kT"][:, h, :, :], in_=bank[:].rearrange("p a r c -> p a (r c)")
             )
-            v_codes = batch.tile([P, PASSES * DV], U32, align_bytes=64)
-            v_scales = batch.tile([P, PASSES * DV], U8, align_bytes=64)
+
+        def quantise_values(b):
+            v_codes = batch.tile([P, PASSES * DV], U32, name="v_codes", align_bytes=64)
+            v_scales = batch.tile([P, PASSES * DV], U8, name="v_scales", align_bytes=64)
             nc.vector.quantize_mx(
                 out=v_codes[:].bitcast(FP8X4),
                 scales=v_scales[:],
-                in_=v_grouped[:].rearrange("p g w t -> p (g w t)"),
+                in_=natural[b]["v_grouped"][:].rearrange("p g w t -> p (g w t)"),
+            )
+            operand[b]["v_codes"] = v_codes
+            operand[b]["v_scales"] = v_scales
+
+        live = {}
+        grouped = {}
+
+        def scores(n):
+            b, i = divmod(n, TILES)
+            qT_tile = operand[b]["qT"][:, i * P : (i + 1) * P]
+            live[n] = {"s": []}
+            for h in range(HALVES):
+                s_bank = psum_s.tile([P, BANK], F32, name="s_bank")
+                nc.tensor.matmul(s_bank[:], lhsT=qT_tile, rhs=operand[b]["kT"][:, h, 0, :], start=True, stop=False)
+                nc.tensor.matmul(s_bank[:], lhsT=qT_tile, rhs=operand[b]["kT"][:, h, 1, :], start=False, stop=True)
+                live[n]["s"].append(s_bank)
+
+        def mask_and_max(n):
+            i = n % TILES
+            s_masked = work.tile([P, T], F32, name="s_masked")
+            for h in range(HALVES):
+                keys = slice(h * BANK, (h + 1) * BANK)
+                nc.vector.tensor_tensor(
+                    out=s_masked[:, keys], in0=live[n]["s"][h][:], in1=mask_bias[:, i, keys], op=ALU.add
+                )
+            neg_max = small.tile([P, 1], F32, name="neg_max")
+            nc.vector.tensor_reduce(out=neg_max[:], in_=s_masked[:], axis=AX.X, op=ALU.max, negate=True)
+            live[n]["s_masked"] = s_masked
+            live[n]["neg_max"] = neg_max
+
+        def exponent(n):
+            e = work.tile([P, T], BF16, name="e")
+            row_sum = small.tile([P, 1], F32, name="row_sum")
+            nc.scalar.activation(
+                out=e[:], in_=live[n]["s_masked"][:], func=ACT.Exp, bias=live[n]["neg_max"][:, 0:1],
+                scale=1.0, accum_out=row_sum[:],
+            )
+            live[n]["e"] = e
+            live[n]["row_sum"] = row_sum
+
+        def invert_sum(n):
+            inv_sum = small.tile([P, 1], F32, name="inv_sum")
+            nc.vector.reciprocal(out=inv_sum[:], in_=live[n]["row_sum"][:])
+            live[n]["inv_sum"] = inv_sum
+
+        def turn(n):
+            e_words = live[n]["e"][:].bitcast(F32)
+            eT_bank = psum_e.tile([P, PASSES * 2, P], F32, name="eT_bank")
+            for c in range(PASSES * 2):
+                nc.tensor.transpose(eT_bank[:, c, :], e_words[:, c * P : (c + 1) * P], ident_f32[:])
+            live[n]["eT_bank"] = eT_bank
+
+        def regroup(n):
+            j, m = divmod(n, GROUP)
+            if m == 0:
+                grouped[j] = {
+                    "e": work.tile([P, GROUP, PASSES * P * PACK], BF16, name="e_grouped", align_bytes=64)
+                }
+            nc.scalar.copy(
+                out=grouped[j]["e"][:, m, :].bitcast(F32).rearrange("p (g q u) -> p g q u", g=PASSES, u=2),
+                in_=live[n]["eT_bank"][:].rearrange("p (g u) q -> p g q u", u=2),
             )
 
-            for i in range(TILES):
-                if b == 0:
-                    load_mask_bias(i)
-                queries = slice(i * P, (i + 1) * P)
+        def quantise(j):
+            e_codes = work.tile([P, GROUP, PASSES, P], U32, name="e_codes", align_bytes=64)
+            e_scales = work.tile([P, GROUP, PASSES, P], U8, name="e_scales", align_bytes=64)
+            nc.vector.quantize_mx(
+                out=e_codes[:].rearrange("p m g q -> p (m g q)").bitcast(FP8X4),
+                scales=e_scales[:].rearrange("p m g q -> p (m g q)"),
+                in_=grouped[j]["e"][:].rearrange("p m c -> p (m c)"),
+            )
+            grouped[j]["codes"] = e_codes
+            grouped[j]["scales"] = e_scales
 
-                s_banks = []
-                bank_max = small.tile([P, HALVES], F32)
-                for h in range(HALVES):
-                    keys = slice(h * BANK, (h + 1) * BANK)
-                    s_bank = psum_s.tile([P, BANK], F32)
-                    s_banks.append(s_bank)
-                    nc.tensor.matmul(s_bank[:], lhsT=qT[:, queries], rhs=hiT[:, keys], start=True, stop=False)
-                    nc.tensor.matmul(s_bank[:], lhsT=qT[:, queries], rhs=loT[:, keys], start=False, stop=False)
-                    for r in range(BANK // P):
-                        nc.tensor.matmul(
-                            s_bank[:, r * P : (r + 1) * P],
-                            lhsT=mask_biasT[:, i, h * (BANK // P) + r, :],
-                            rhs=ident_f32[:],
-                            is_transpose=True,
-                            start=False,
-                            stop=(r == BANK // P - 1),
-                        )
-                    nc.vector.tensor_reduce(out=bank_max[:, h : h + 1], in_=s_bank[:], axis=AX.X, op=ALU.max)
-                neg_max = small.tile([P, 1], F32)
-                nc.vector.tensor_reduce(out=neg_max[:], in_=bank_max[:], axis=AX.X, op=ALU.max, negate=True)
-                e = work.tile([P, T], BF16)
-                bank_sum = small.tile([P, HALVES], F32)
-                for h in range(HALVES):
-                    nc.scalar.activation(
-                        out=e[:, h * BANK : (h + 1) * BANK], in_=s_banks[h][:], func=ACT.Exp,
-                        bias=neg_max[:, 0:1], scale=1.0, accum_out=bank_sum[:, h : h + 1],
-                    )
-                row_sum = small.tile([P, 1], F32)
-                nc.vector.tensor_reduce(out=row_sum[:], in_=bank_sum[:], axis=AX.X, op=ALU.add)
-                inv_sum = small.tile([P, 1], F32)
-                nc.vector.reciprocal(out=inv_sum[:], in_=row_sum[:])
-
-                e_words = e[:].bitcast(F32)
-                eT_bank = psum_e.tile([P, PASSES * 2, P], F32)
-                for c in range(PASSES * 2):
-                    nc.tensor.transpose(eT_bank[:, c, :], e_words[:, c * P : (c + 1) * P], ident_f32[:])
-                e_grouped = work.tile([P, PASSES * P * PACK], BF16, align_bytes=64)
-                nc.scalar.copy(
-                    out=e_grouped[:].bitcast(F32).rearrange("p (g q u) -> p g q u", g=PASSES, u=2),
-                    in_=eT_bank[:].rearrange("p (g u) q -> p g q u", u=2),
-                )
-                e_codes = work.tile([P, PASSES * P], U32, align_bytes=64)
-                e_scales = work.tile([P, PASSES * P], U8, align_bytes=64)
-                nc.vector.quantize_mx(out=e_codes[:].bitcast(FP8X4), scales=e_scales[:], in_=e_grouped[:])
-
-                o_bank = psum_o.tile([P, DV], F32)
+        def product(j):
+            ops = operand[(j * GROUP) // TILES]
+            o_bank = psum_o.tile([P, GROUP, DV], F32, name="o_bank")
+            for m in range(GROUP):
                 for g in range(PASSES):
                     nc.tensor.matmul_mx(
-                        out=o_bank[:],
-                        lhsT=e_codes[:, g * P : (g + 1) * P].bitcast(FP8X4),
-                        lhsT_scale=e_scales[:, g * P : (g + 1) * P],
-                        rhs=v_codes[:, g * DV : (g + 1) * DV].bitcast(FP8X4),
-                        rhs_scale=v_scales[:, g * DV : (g + 1) * DV],
+                        out=o_bank[:, m, :],
+                        lhsT=grouped[j]["codes"][:, m, g, :].bitcast(FP8X4),
+                        lhsT_scale=grouped[j]["scales"][:, m, g, :],
+                        rhs=ops["v_codes"][:, g * DV : (g + 1) * DV].bitcast(FP8X4),
+                        rhs_scale=ops["v_scales"][:, g * DV : (g + 1) * DV],
                         start=(g == 0),
                         stop=(g == PASSES - 1),
                     )
-                o_sb = work.tile([P, DV], F32)
-                nc.scalar.activation(out=o_sb[:], in_=o_bank[:], func=ACT.Copy, scale=inv_sum[:, 0:1])
-                nc.sync.dma_start(out=out[b, queries, :], in_=o_sb[:])
+            grouped[j]["o_bank"] = o_bank
+
+        def finish(j):
+            b, i = divmod(j * GROUP, TILES)
+            o_sb = work.tile([P, GROUP, DV], F32, name="o_sb")
+            for m in range(GROUP):
+                nc.scalar.activation(
+                    out=o_sb[:, m, :], in_=grouped[j]["o_bank"][:, m, :], func=ACT.Copy,
+                    scale=live[j * GROUP + m]["inv_sum"][:, 0:1],
+                )
+            nc.sync.dma_start(
+                out=out[b, i * P : (i + GROUP) * P, :].rearrange("(m p) w -> p m w", p=P), in_=o_sb[:]
+            )
+
+        load_batch(0)
+        load_mask(0)
+        load_values(0)
+        load_batch(1)
+        load_mask(1)
+        load_values(1)
+        blend_keys(0, nc.vector)
+        group_values(0, nc.gpsimd)
+        blend_keys(1, nc.gpsimd)
+        group_values(1, nc.gpsimd)
+        turn_queries(0)
+        turn_keys(0, 0)
+        convert_mask(0)
+        turn_keys(0, 1)
+        quantise_values(0)
+        scores(0)
+
+        def on(stage, n):
+            if 0 <= n < N_TILES:
+                stage(n)
+
+        def on_group(stage, last):
+            if 0 <= last < N_TILES and last % GROUP == GROUP - 1:
+                stage(last // GROUP)
+
+        for t in range(N_TILES + 3):
+            b, i = divmod(t, TILES)
+            if i == 0 and b + 2 < B:
+                load_batch(b + 2)
+                load_values(b + 2)
+                blend_keys(b + 2, nc.gpsimd)
+                group_values(b + 2, nc.gpsimd)
+            if t + 2 < TILES:
+                load_mask(t + 2)
+            on_group(product, t - 3)
+            on(scores, t + 1)
+            on(exponent, t - 1)
+            on(regroup, t - 2)
+            on(turn, t - 1)
+            on_group(finish, t - 3)
+            on(mask_and_max, t)
+            on_group(quantise, t - 2)
+            on(invert_sum, t - 1)
+            if t + 1 < TILES:
+                convert_mask(t + 1)
+            if b + 1 < B:
+                if i == 1:
+                    turn_queries(b + 1)
+                if i == 3:
+                    turn_keys(b + 1, 0)
+                if i == 5:
+                    turn_keys(b + 1, 1)
+                if i == 6:
+                    quantise_values(b + 1)

@@ -70,7 +70,7 @@ def tile_dualmodehead_t_kernel(tc, q, k, v, mask, mode, out):
         mask_raw = {}
 
         def load_mask(i):
-            mask_raw[i] = loads.tile([P, T, MASK_WORDS], I32, name="mask_raw")
+            mask_raw[i] = loads.tile([P, T, MASK_WORDS], I32, name="mask_raw", bufs=3)
             nc.sync.dma_start(
                 out=mask_raw[i][:].rearrange("p k w -> p (k w)"), in_=mask_rows[i * P : (i + 1) * P, :]
             )
@@ -100,12 +100,13 @@ def tile_dualmodehead_t_kernel(tc, q, k, v, mask, mode, out):
             )
             natural[b]["v"] = v_raw
 
-        def blend_keys(b, engine):
+        def blend_keys(b, engines):
             k_nat = natural[b]["k"]
             k_meson = loads.tile([P, TILES, D], F32, name="k_meson")
             k_baryon = loads.tile([P, TILES, D], F32, name="k_baryon")
             k_parts = loads.tile([P, 2, TILES, D], BF16, name="k_parts")
             for h in range(HALVES):
+                engine = engines[h]
                 js = slice(h * BLOCKS, (h + 1) * BLOCKS)
                 engine.tensor_scalar(
                     out=k_meson[:, js, :], in0=k_nat[:, js, :], scalar1=c_meson[:, 0:1], scalar2=0.0,
@@ -183,7 +184,7 @@ def tile_dualmodehead_t_kernel(tc, q, k, v, mask, mode, out):
                 nc.tensor.matmul(s_bank[:], lhsT=qT_tile, rhs=operand[b]["kT"][:, h, 1, :], start=False, stop=True)
                 live[n]["s"].append(s_bank)
 
-        def mask_and_max(n):
+        def add_mask(n):
             i = n % TILES
             s_masked = work.tile([P, T], F32, name="s_masked")
             for h in range(HALVES):
@@ -191,25 +192,30 @@ def tile_dualmodehead_t_kernel(tc, q, k, v, mask, mode, out):
                 nc.vector.tensor_tensor(
                     out=s_masked[:, keys], in0=live[n]["s"][h][:], in1=mask_bias[:, i, keys], op=ALU.add
                 )
-            neg_max = small.tile([P, 1], F32, name="neg_max")
-            nc.vector.tensor_reduce(out=neg_max[:], in_=s_masked[:], axis=AX.X, op=ALU.max, negate=True)
             live[n]["s_masked"] = s_masked
+
+        def row_max(n):
+            neg_max = small.tile([P, 1], F32, name="neg_max")
+            nc.vector.tensor_reduce(
+                out=neg_max[:], in_=live[n]["s_masked"][:], axis=AX.X, op=ALU.max, negate=True
+            )
             live[n]["neg_max"] = neg_max
 
         def exponent(n):
+            j, m = divmod(n, GROUP)
+            if m == 0:
+                grouped[j] = {"row_sum": small.tile([P, GROUP], F32, name="row_sum")}
             e = work.tile([P, T], BF16, name="e")
-            row_sum = small.tile([P, 1], F32, name="row_sum")
             nc.scalar.activation(
                 out=e[:], in_=live[n]["s_masked"][:], func=ACT.Exp, bias=live[n]["neg_max"][:, 0:1],
-                scale=1.0, accum_out=row_sum[:],
+                scale=1.0, accum_out=grouped[j]["row_sum"][:, m : m + 1],
             )
             live[n]["e"] = e
-            live[n]["row_sum"] = row_sum
 
-        def invert_sum(n):
-            inv_sum = small.tile([P, 1], F32, name="inv_sum")
-            nc.vector.reciprocal(out=inv_sum[:], in_=live[n]["row_sum"][:])
-            live[n]["inv_sum"] = inv_sum
+        def invert_sums(j):
+            inv_sum = small.tile([P, GROUP], F32, name="inv_sum")
+            nc.vector.reciprocal(out=inv_sum[:], in_=grouped[j]["row_sum"][:])
+            grouped[j]["inv_sum"] = inv_sum
 
         def turn(n):
             e_words = live[n]["e"][:].bitcast(F32)
@@ -221,9 +227,7 @@ def tile_dualmodehead_t_kernel(tc, q, k, v, mask, mode, out):
         def regroup(n):
             j, m = divmod(n, GROUP)
             if m == 0:
-                grouped[j] = {
-                    "e": work.tile([P, GROUP, PASSES * P * PACK], BF16, name="e_grouped", align_bytes=64)
-                }
+                grouped[j]["e"] = work.tile([P, GROUP, PASSES * P * PACK], BF16, name="e_grouped", align_bytes=64)
             nc.scalar.copy(
                 out=grouped[j]["e"][:, m, :].bitcast(F32).rearrange("p (g q u) -> p g q u", g=PASSES, u=2),
                 in_=live[n]["eT_bank"][:].rearrange("p (g u) q -> p g q u", u=2),
@@ -262,7 +266,7 @@ def tile_dualmodehead_t_kernel(tc, q, k, v, mask, mode, out):
             for m in range(GROUP):
                 nc.scalar.activation(
                     out=o_sb[:, m, :], in_=grouped[j]["o_bank"][:, m, :], func=ACT.Copy,
-                    scale=live[j * GROUP + m]["inv_sum"][:, 0:1],
+                    scale=grouped[j]["inv_sum"][:, m : m + 1],
                 )
             nc.sync.dma_start(
                 out=out[b, i * P : (i + GROUP) * P, :].rearrange("(m p) w -> p m w", p=P), in_=o_sb[:]
@@ -271,19 +275,23 @@ def tile_dualmodehead_t_kernel(tc, q, k, v, mask, mode, out):
         load_batch(0)
         load_mask(0)
         load_values(0)
-        load_batch(1)
         load_mask(1)
+        load_batch(1)
         load_values(1)
-        blend_keys(0, nc.vector)
+        load_mask(2)
+        blend_keys(0, [nc.vector, nc.gpsimd])
         group_values(0, nc.gpsimd)
-        blend_keys(1, nc.gpsimd)
+        blend_keys(1, [nc.gpsimd, nc.gpsimd])
         group_values(1, nc.gpsimd)
         turn_queries(0)
         turn_keys(0, 0)
         convert_mask(0)
         turn_keys(0, 1)
-        quantise_values(0)
+        convert_mask(1)
         scores(0)
+        scores(1)
+        add_mask(0)
+        quantise_values(0)
 
         def on(stage, n):
             if 0 <= n < N_TILES:
@@ -298,21 +306,22 @@ def tile_dualmodehead_t_kernel(tc, q, k, v, mask, mode, out):
             if i == 0 and b + 2 < B:
                 load_batch(b + 2)
                 load_values(b + 2)
-                blend_keys(b + 2, nc.gpsimd)
+                blend_keys(b + 2, [nc.gpsimd, nc.gpsimd])
                 group_values(b + 2, nc.gpsimd)
-            if t + 2 < TILES:
-                load_mask(t + 2)
+            if t + 3 < TILES:
+                load_mask(t + 3)
             on_group(product, t - 3)
-            on(scores, t + 1)
+            on(scores, t + 2)
             on(exponent, t - 1)
             on(regroup, t - 2)
             on(turn, t - 1)
             on_group(finish, t - 3)
-            on(mask_and_max, t)
+            on(add_mask, t + 1)
+            on(row_max, t)
             on_group(quantise, t - 2)
-            on(invert_sum, t - 1)
-            if t + 1 < TILES:
-                convert_mask(t + 1)
+            on_group(invert_sums, t - 1)
+            if t + 2 < TILES:
+                convert_mask(t + 2)
             if b + 1 < B:
                 if i == 1:
                     turn_queries(b + 1)

@@ -45,7 +45,6 @@ def tile_dualmodehead_t_kernel(tc, q, k, v, mask, mode, out):
         psum_e = ctx.enter_context(tc.psum_pool(name="psum_e", bufs=2))
         psum_o = ctx.enter_context(tc.psum_pool(name="psum_o", bufs=1))
         psum_t = ctx.enter_context(tc.psum_pool(name="psum_t", bufs=1))
-        ctx.enter_context(tc.manual_schedule())
 
         ident_bf = const.tile([P, P], BF16)
         make_identity(nc, ident_bf[:])

@@ -39,12 +39,13 @@ def tile_dualmodehead_t_kernel(tc, q, k, v, mask, mode, out):
         const = ctx.enter_context(tc.tile_pool(name="const", bufs=1))
         loads = ctx.enter_context(tc.tile_pool(name="loads", bufs=2))
         batch = ctx.enter_context(tc.tile_pool(name="batch", bufs=2))
-        work = ctx.enter_context(tc.tile_pool(name="work", bufs=3))
-        small = ctx.enter_context(tc.tile_pool(name="small", bufs=6))
+        work = ctx.enter_context(tc.tile_pool(name="work", bufs=4))
+        small = ctx.enter_context(tc.tile_pool(name="small", bufs=8))
         psum_s = ctx.enter_context(tc.psum_pool(name="psum_s", bufs=4))
         psum_e = ctx.enter_context(tc.psum_pool(name="psum_e", bufs=2))
         psum_o = ctx.enter_context(tc.psum_pool(name="psum_o", bufs=1))
         psum_t = ctx.enter_context(tc.psum_pool(name="psum_t", bufs=1))
+        ctx.enter_context(tc.manual_schedule())
 
         ident_bf = const.tile([P, P], BF16)
         make_identity(nc, ident_bf[:])
@@ -76,8 +77,12 @@ def tile_dualmodehead_t_kernel(tc, q, k, v, mask, mode, out):
 
         def convert_mask(i):
             nc.scalar.activation(
-                out=mask_bias[:, i, :], in_=mask_raw[i][:].bitcast(U32)[:, :, 0], func=ACT.Copy,
+                out=mask_bias[:, i, 0:BANK], in_=mask_raw[i][:].bitcast(U32)[:, 0:BANK, 0], func=ACT.Copy,
                 scale=-MASKED, bias=MASKED,
+            )
+            nc.vector.tensor_scalar(
+                out=mask_bias[:, i, BANK:T], in0=mask_raw[i][:, BANK:T, 0], scalar1=-MASKED,
+                scalar2=MASKED, op0=ALU.mult, op1=ALU.add,
             )
 
         natural = {}
@@ -300,7 +305,7 @@ def tile_dualmodehead_t_kernel(tc, q, k, v, mask, mode, out):
             if 0 <= last < N_TILES and last % GROUP == GROUP - 1:
                 stage(last // GROUP)
 
-        for t in range(N_TILES + 3):
+        for t in range(N_TILES + 6):
             b, i = divmod(t, TILES)
             if i == 0 and b + 2 < B:
                 load_batch(b + 2)
@@ -309,16 +314,16 @@ def tile_dualmodehead_t_kernel(tc, q, k, v, mask, mode, out):
                 group_values(b + 2, nc.gpsimd)
             if t + 3 < TILES:
                 load_mask(t + 3)
-            on_group(product, t - 3)
+            on_group(product, t - 5)
             on(scores, t + 2)
             on(exponent, t - 1)
-            on(regroup, t - 2)
-            on(turn, t - 1)
-            on_group(finish, t - 3)
+            on(regroup, t - 3)
+            on(turn, t - 2)
+            on_group(finish, t - 5)
             on(add_mask, t + 1)
             on(row_max, t)
-            on_group(quantise, t - 2)
-            on_group(invert_sums, t - 1)
+            on_group(quantise, t - 4)
+            on_group(invert_sums, t - 4)
             if t + 2 < TILES:
                 convert_mask(t + 2)
             if b + 1 < B:

@@ -23,6 +23,7 @@ BLOCKS = BANK // P
 PACK = 4
 K_PASS = P * PACK
 PASSES = T // K_PASS
+ON_TENSOR = (1, 4)
 GROUP = 2
 MASK_WORDS = 2
 MASKED = -(2.0**100)
@@ -41,10 +42,9 @@ def tile_dualmodehead_t_kernel(tc, q, k, v, mask, mode, out):
         batch = ctx.enter_context(tc.tile_pool(name="batch", bufs=2))
         work = ctx.enter_context(tc.tile_pool(name="work", bufs=4))
         small = ctx.enter_context(tc.tile_pool(name="small", bufs=8))
-        psum_s = ctx.enter_context(tc.psum_pool(name="psum_s", bufs=4))
-        psum_e = ctx.enter_context(tc.psum_pool(name="psum_e", bufs=2))
+        psum_s = ctx.enter_context(tc.psum_pool(name="psum_s", bufs=5))
+        psum_t = ctx.enter_context(tc.psum_pool(name="psum_t", bufs=2))
         psum_o = ctx.enter_context(tc.psum_pool(name="psum_o", bufs=1))
-        psum_t = ctx.enter_context(tc.psum_pool(name="psum_t", bufs=1))
         ctx.enter_context(tc.manual_schedule())
 
         ident_bf = const.tile([P, P], BF16)
@@ -70,7 +70,7 @@ def tile_dualmodehead_t_kernel(tc, q, k, v, mask, mode, out):
         mask_raw = {}
 
         def load_mask(i):
-            mask_raw[i] = loads.tile([P, T, MASK_WORDS], I32, name="mask_raw", bufs=3)
+            mask_raw[i] = loads.tile([P, T, MASK_WORDS], I32, name="mask_raw", bufs=4)
             nc.sync.dma_start(
                 out=mask_raw[i][:].rearrange("p k w -> p (k w)"), in_=mask_rows[i * P : (i + 1) * P, :]
             )
@@ -178,6 +178,9 @@ def tile_dualmodehead_t_kernel(tc, q, k, v, mask, mode, out):
         live = {}
         grouped = {}
 
+        def mask_on_tensor(n, h):
+            return h == HALVES - 1 and n % 5 in ON_TENSOR
+
         def scores(n):
             b, i = divmod(n, TILES)
             qT_tile = operand[b]["qT"][:, i * P : (i + 1) * P]
@@ -185,24 +188,41 @@ def tile_dualmodehead_t_kernel(tc, q, k, v, mask, mode, out):
             for h in range(HALVES):
                 s_bank = psum_s.tile([P, BANK], F32, name="s_bank")
                 nc.tensor.matmul(s_bank[:], lhsT=qT_tile, rhs=operand[b]["kT"][:, h, 0, :], start=True, stop=False)
-                nc.tensor.matmul(s_bank[:], lhsT=qT_tile, rhs=operand[b]["kT"][:, h, 1, :], start=False, stop=True)
+                nc.tensor.matmul(
+                    s_bank[:], lhsT=qT_tile, rhs=operand[b]["kT"][:, h, 1, :], start=False,
+                    stop=not mask_on_tensor(n, h),
+                )
+                if mask_on_tensor(n, h):
+                    nc.tensor.matmul(
+                        s_bank[:], lhsT=ident_bf[:], rhs=mask_bias[:, i, h * BANK : (h + 1) * BANK],
+                        start=False, stop=True,
+                    )
                 live[n]["s"].append(s_bank)
 
         def add_mask(n):
             i = n % TILES
             s_masked = work.tile([P, T], F32, name="s_masked")
             for h in range(HALVES):
+                if mask_on_tensor(n, h):
+                    continue
                 keys = slice(h * BANK, (h + 1) * BANK)
                 nc.vector.tensor_tensor(
                     out=s_masked[:, keys], in0=live[n]["s"][h][:], in1=mask_bias[:, i, keys], op=ALU.add
                 )
             live[n]["s_masked"] = s_masked
 
+        def fold(n):
+            if mask_on_tensor(n, 1):
+                folded = work.tile([P, BANK], F32, name="folded", bufs=2)
+                nc.vector.tensor_tensor(
+                    out=folded[:], in0=live[n]["s"][1][:], in1=live[n]["s_masked"][:, 0:BANK], op=ALU.max
+                )
+                live[n]["folded"] = folded
+
         def row_max(n):
             neg_max = small.tile([P, 1], F32, name="neg_max")
-            nc.vector.tensor_reduce(
-                out=neg_max[:], in_=live[n]["s_masked"][:], axis=AX.X, op=ALU.max, negate=True
-            )
+            source = live[n]["folded"] if mask_on_tensor(n, 1) else live[n]["s_masked"]
+            nc.vector.tensor_reduce(out=neg_max[:], in_=source[:], axis=AX.X, op=ALU.max, negate=True)
             live[n]["neg_max"] = neg_max
 
         def exponent(n):
@@ -210,10 +230,25 @@ def tile_dualmodehead_t_kernel(tc, q, k, v, mask, mode, out):
             if m == 0:
                 grouped[j] = {"row_sum": small.tile([P, GROUP], F32, name="row_sum")}
             e = work.tile([P, T], BF16, name="e")
-            nc.scalar.activation(
-                out=e[:], in_=live[n]["s_masked"][:], func=ACT.Exp, bias=live[n]["neg_max"][:, 0:1],
-                scale=1.0, accum_out=grouped[j]["row_sum"][:, m : m + 1],
-            )
+            row_sum = grouped[j]["row_sum"][:, m : m + 1]
+            neg_max = live[n]["neg_max"][:, 0:1]
+            if mask_on_tensor(n, 1):
+                half_sum = small.tile([P, HALVES], F32, name="half_sum")
+                nc.scalar.activation(
+                    out=e[:, BANK:T], in_=live[n]["s"][1][:], func=ACT.Exp, bias=neg_max, scale=1.0,
+                    accum_out=half_sum[:, 1:2],
+                )
+                nc.scalar.activation(
+                    out=e[:, 0:BANK], in_=live[n]["s_masked"][:, 0:BANK], func=ACT.Exp, bias=neg_max, scale=1.0,
+                    accum_out=half_sum[:, 0:1],
+                )
+                nc.scalar.activation(
+                    out=row_sum, in_=half_sum[:, 0:1], func=ACT.Identity, bias=half_sum[:, 1:2], scale=1.0
+                )
+            else:
+                nc.scalar.activation(
+                    out=e[:], in_=live[n]["s_masked"][:], func=ACT.Exp, bias=neg_max, scale=1.0, accum_out=row_sum
+                )
             live[n]["e"] = e
 
         def invert_sums(j):
@@ -223,7 +258,7 @@ def tile_dualmodehead_t_kernel(tc, q, k, v, mask, mode, out):
 
         def turn(n):
             e_words = live[n]["e"][:].bitcast(F32)
-            eT_bank = psum_e.tile([P, PASSES * 2, P], F32, name="eT_bank")
+            eT_bank = psum_t.tile([P, PASSES * 2, P], F32, name="eT_bank", tag="bank_t")
             for c in range(PASSES * 2):
                 nc.tensor.transpose(eT_bank[:, c, :], e_words[:, c * P : (c + 1) * P], ident_f32[:])
             live[n]["eT_bank"] = eT_bank
@@ -283,6 +318,7 @@ def tile_dualmodehead_t_kernel(tc, q, k, v, mask, mode, out):
         load_batch(1)
         load_values(1)
         load_mask(2)
+        load_mask(3)
         blend_keys(0, [nc.vector, nc.gpsimd])
         group_values(0, nc.gpsimd)
         blend_keys(1, [nc.gpsimd, nc.gpsimd])
@@ -296,6 +332,7 @@ def tile_dualmodehead_t_kernel(tc, q, k, v, mask, mode, out):
         scores(1)
         add_mask(0)
         quantise_values(0)
+        convert_mask(2)
 
         def on(stage, n):
             if 0 <= n < N_TILES:
@@ -312,20 +349,21 @@ def tile_dualmodehead_t_kernel(tc, q, k, v, mask, mode, out):
                 load_values(b + 2)
                 blend_keys(b + 2, [nc.gpsimd, nc.gpsimd])
                 group_values(b + 2, nc.gpsimd)
-            if t + 3 < TILES:
-                load_mask(t + 3)
+            if t + 4 < TILES:
+                load_mask(t + 4)
             on_group(product, t - 5)
-            on(scores, t + 2)
             on(exponent, t - 1)
             on(regroup, t - 3)
             on(turn, t - 2)
+            on(scores, t + 2)
             on_group(finish, t - 5)
+            on(fold, t)
             on(add_mask, t + 1)
             on(row_max, t)
             on_group(quantise, t - 4)
             on_group(invert_sums, t - 4)
-            if t + 2 < TILES:
-                convert_mask(t + 2)
+            if t + 3 < TILES:
+                convert_mask(t + 3)
             if b + 1 < B:
                 if i == 1:
                     turn_queries(b + 1)

@@ -23,7 +23,7 @@ BLOCKS = BANK // P
 PACK = 4
 K_PASS = P * PACK
 PASSES = T // K_PASS
-ON_TENSOR = (1, 4)
+FIRST_ON_TENSOR = 8
 GROUP = 2
 MASK_WORDS = 2
 MASKED = -(2.0**100)
@@ -42,8 +42,10 @@ def tile_dualmodehead_t_kernel(tc, q, k, v, mask, mode, out):
         batch = ctx.enter_context(tc.tile_pool(name="batch", bufs=2))
         work = ctx.enter_context(tc.tile_pool(name="work", bufs=4))
         small = ctx.enter_context(tc.tile_pool(name="small", bufs=8))
-        psum_s = ctx.enter_context(tc.psum_pool(name="psum_s", bufs=5))
-        psum_t = ctx.enter_context(tc.psum_pool(name="psum_t", bufs=2))
+        psum_a = ctx.enter_context(tc.psum_pool(name="psum_a", bufs=2))
+        psum_b = ctx.enter_context(tc.psum_pool(name="psum_b", bufs=3))
+        psum_t = ctx.enter_context(tc.psum_pool(name="psum_t", bufs=1))
+        psum_e = ctx.enter_context(tc.psum_pool(name="psum_e", bufs=1))
         psum_o = ctx.enter_context(tc.psum_pool(name="psum_o", bufs=1))
         ctx.enter_context(tc.manual_schedule())
 
@@ -67,10 +69,12 @@ def tile_dualmodehead_t_kernel(tc, q, k, v, mask, mode, out):
 
         mask_bias = const.tile([P, TILES, T], BF16)
 
+        mask_turned = const.tile([P, TILES, BLOCKS, P], F32)
+
         mask_raw = {}
 
         def load_mask(i):
-            mask_raw[i] = loads.tile([P, T, MASK_WORDS], I32, name="mask_raw", bufs=4)
+            mask_raw[i] = loads.tile([P, T, MASK_WORDS], I32, name="mask_raw", bufs=6)
             nc.sync.dma_start(
                 out=mask_raw[i][:].rearrange("p k w -> p (k w)"), in_=mask_rows[i * P : (i + 1) * P, :]
             )
@@ -83,6 +87,19 @@ def tile_dualmodehead_t_kernel(tc, q, k, v, mask, mode, out):
             nc.vector.tensor_scalar(
                 out=mask_bias[:, i, BANK:T], in0=mask_raw[i][:, BANK:T, 0], scalar1=-MASKED,
                 scalar2=MASKED, op0=ALU.mult, op1=ALU.add,
+            )
+
+        mask_banks = {}
+
+        def turn_mask(i):
+            bank = psum_t.tile([P, BLOCKS, P], BF16, name="bank_m", tag="bank_t")
+            for r in range(BLOCKS):
+                nc.tensor.transpose(bank[:, r, :], mask_bias[:, i, BANK + r * P : BANK + (r + 1) * P], ident_bf[:])
+            mask_banks[i] = bank
+
+        def keep_mask(i):
+            nc.scalar.activation(
+                out=mask_turned[:, i, :, :], in_=mask_banks[i][:], func=ACT.Copy, scale=1.0
             )
 
         natural = {}
@@ -147,8 +164,11 @@ def tile_dualmodehead_t_kernel(tc, q, k, v, mask, mode, out):
             bank = psum_t.tile([P, T], BF16, name="bank_q", tag="bank_t")
             for j in range(TILES):
                 nc.tensor.transpose(bank[:, j * P : (j + 1) * P], natural[b]["q"][:, j, :], ident_bf[:])
+            operand[b]["bank_q"] = bank
+
+        def keep_queries(b):
             qT = batch.tile([P, T], BF16, name="qT")
-            nc.scalar.copy(out=qT[:], in_=bank[:])
+            nc.scalar.copy(out=qT[:], in_=operand[b]["bank_q"][:])
             operand[b]["qT"] = qT
 
         def turn_keys(b, h):
@@ -160,8 +180,11 @@ def tile_dualmodehead_t_kernel(tc, q, k, v, mask, mode, out):
                     nc.tensor.transpose(
                         bank[:, part, r, :], natural[b]["k_parts"][:, part, h * BLOCKS + r, :], ident_bf[:]
                     )
+            operand[b]["bank_k"] = bank
+
+        def keep_keys(b, h):
             nc.scalar.copy(
-                out=operand[b]["kT"][:, h, :, :], in_=bank[:].rearrange("p a r c -> p a (r c)")
+                out=operand[b]["kT"][:, h, :, :], in_=operand[b]["bank_k"][:].rearrange("p a r c -> p a (r c)")
             )
 
         def quantise_values(b):
@@ -178,25 +201,29 @@ def tile_dualmodehead_t_kernel(tc, q, k, v, mask, mode, out):
         live = {}
         grouped = {}
 
+        def on_tensor(n):
+            return n >= FIRST_ON_TENSOR
+
         def mask_on_tensor(n, h):
-            return h == HALVES - 1 and n % 5 in ON_TENSOR
+            return h == HALVES - 1 and on_tensor(n)
 
         def scores(n):
             b, i = divmod(n, TILES)
             qT_tile = operand[b]["qT"][:, i * P : (i + 1) * P]
             live[n] = {"s": []}
             for h in range(HALVES):
-                s_bank = psum_s.tile([P, BANK], F32, name="s_bank")
+                s_bank = (psum_a, psum_b)[h].tile([P, BANK], F32, name="s_bank")
                 nc.tensor.matmul(s_bank[:], lhsT=qT_tile, rhs=operand[b]["kT"][:, h, 0, :], start=True, stop=False)
                 nc.tensor.matmul(
                     s_bank[:], lhsT=qT_tile, rhs=operand[b]["kT"][:, h, 1, :], start=False,
                     stop=not mask_on_tensor(n, h),
                 )
                 if mask_on_tensor(n, h):
-                    nc.tensor.matmul(
-                        s_bank[:], lhsT=ident_bf[:], rhs=mask_bias[:, i, h * BANK : (h + 1) * BANK],
-                        start=False, stop=True,
-                    )
+                    for r in range(BLOCKS):
+                        nc.tensor.matmul(
+                            s_bank[:, r * P : (r + 1) * P], lhsT=mask_turned[:, i, r, :], rhs=ident_f32[:],
+                            start=False, stop=(r == BLOCKS - 1), is_transpose=True,
+                        )
                 live[n]["s"].append(s_bank)
 
         def add_mask(n):
@@ -242,14 +269,21 @@ def tile_dualmodehead_t_kernel(tc, q, k, v, mask, mode, out):
                     out=e[:, 0:BANK], in_=live[n]["s_masked"][:, 0:BANK], func=ACT.Exp, bias=neg_max, scale=1.0,
                     accum_out=half_sum[:, 0:1],
                 )
-                nc.scalar.activation(
-                    out=row_sum, in_=half_sum[:, 0:1], func=ACT.Identity, bias=half_sum[:, 1:2], scale=1.0
-                )
+                live[n]["half_sum"] = half_sum
             else:
                 nc.scalar.activation(
                     out=e[:], in_=live[n]["s_masked"][:], func=ACT.Exp, bias=neg_max, scale=1.0, accum_out=row_sum
                 )
             live[n]["e"] = e
+
+        def add_half_sums(n):
+            if on_tensor(n):
+                j, m = divmod(n, GROUP)
+                half_sum = live[n]["half_sum"]
+                nc.scalar.activation(
+                    out=grouped[j]["row_sum"][:, m : m + 1], in_=half_sum[:, 0:1], func=ACT.Identity,
+                    bias=half_sum[:, 1:2], scale=1.0,
+                )
 
         def invert_sums(j):
             inv_sum = small.tile([P, GROUP], F32, name="inv_sum")
@@ -258,7 +292,7 @@ def tile_dualmodehead_t_kernel(tc, q, k, v, mask, mode, out):
 
         def turn(n):
             e_words = live[n]["e"][:].bitcast(F32)
-            eT_bank = psum_t.tile([P, PASSES * 2, P], F32, name="eT_bank", tag="bank_t")
+            eT_bank = psum_e.tile([P, PASSES * 2, P], F32, name="eT_bank")
             for c in range(PASSES * 2):
                 nc.tensor.transpose(eT_bank[:, c, :], e_words[:, c * P : (c + 1) * P], ident_f32[:])
             live[n]["eT_bank"] = eT_bank
@@ -313,26 +347,29 @@ def tile_dualmodehead_t_kernel(tc, q, k, v, mask, mode, out):
 
         load_batch(0)
         load_mask(0)
-        load_values(0)
         load_mask(1)
-        load_batch(1)
-        load_values(1)
         load_mask(2)
+        load_values(0)
         load_mask(3)
+        load_batch(1)
+        load_mask(4)
+        load_values(1)
+        load_mask(5)
         blend_keys(0, [nc.vector, nc.gpsimd])
         group_values(0, nc.gpsimd)
         blend_keys(1, [nc.gpsimd, nc.gpsimd])
         group_values(1, nc.gpsimd)
         turn_queries(0)
+        keep_queries(0)
         turn_keys(0, 0)
+        keep_keys(0, 0)
         convert_mask(0)
         turn_keys(0, 1)
+        keep_keys(0, 1)
         convert_mask(1)
         scores(0)
         scores(1)
         add_mask(0)
-        quantise_values(0)
-        convert_mask(2)
 
         def on(stage, n):
             if 0 <= n < N_TILES:
@@ -344,32 +381,45 @@ def tile_dualmodehead_t_kernel(tc, q, k, v, mask, mode, out):
 
         for t in range(N_TILES + 6):
             b, i = divmod(t, TILES)
-            if i == 0 and b + 2 < B:
+            if i == 4 and b + 2 < B:
                 load_batch(b + 2)
                 load_values(b + 2)
                 blend_keys(b + 2, [nc.gpsimd, nc.gpsimd])
                 group_values(b + 2, nc.gpsimd)
-            if t + 4 < TILES:
-                load_mask(t + 4)
+            if t + 6 < TILES:
+                load_mask(t + 6)
             on_group(product, t - 5)
             on(exponent, t - 1)
-            on(regroup, t - 3)
-            on(turn, t - 2)
             on(scores, t + 2)
+            on(regroup, t - 3)
+            on(add_half_sums, t - 1)
+            on(turn, t - 2)
             on_group(finish, t - 5)
             on(fold, t)
             on(add_mask, t + 1)
             on(row_max, t)
             on_group(quantise, t - 4)
             on_group(invert_sums, t - 4)
-            if t + 3 < TILES:
-                convert_mask(t + 3)
+            if t + 2 < TILES:
+                convert_mask(t + 2)
+            if t == 3:
+                quantise_values(0)
             if b + 1 < B:
                 if i == 1:
-                    turn_queries(b + 1)
+                    keep_queries(b + 1)
                 if i == 3:
-                    turn_keys(b + 1, 0)
+                    keep_keys(b + 1, 0)
                 if i == 5:
-                    turn_keys(b + 1, 1)
+                    keep_keys(b + 1, 1)
                 if i == 6:
                     quantise_values(b + 1)
+            if 2 <= t < TILES + 2:
+                turn_mask(t - 2)
+                keep_mask(t - 2)
+            if b + 1 < B:
+                if i == 0:
+                    turn_queries(b + 1)
+                if i == 2:
+                    turn_keys(b + 1, 0)
+                if i == 4:
+                    turn_keys(b + 1, 1)

@@ -80,19 +80,14 @@ def tile_dualmodehead_t_kernel(tc, q, k, v, mask, mode, out):
             )
 
         def convert_mask(i):
-            nc.scalar.activation(
-                out=mask_bias[:, i, 0:BANK], in_=mask_raw[i][:].bitcast(U32)[:, 0:BANK, 0], func=ACT.Copy,
-                scale=-MASKED, bias=MASKED,
-            )
             nc.vector.tensor_scalar(
-                out=mask_bias[:, i, BANK:T], in0=mask_raw[i][:, BANK:T, 0], scalar1=-MASKED,
-                scalar2=MASKED, op0=ALU.mult, op1=ALU.add,
+                out=mask_bias[:, i, :], in0=mask_raw[i][:, :, 0], scalar1=-MASKED, scalar2=MASKED, op0=ALU.mult, op1=ALU.add
             )
 
         mask_banks = {}
 
-        def turn_mask(i):
-            bank = psum_t.tile([P, BLOCKS, P], BF16, name="bank_m", tag="bank_t")
+        def turn_mask(i, pool, tag):
+            bank = pool.tile([P, BLOCKS, P], BF16, name="bank_m", tag=tag)
             for r in range(BLOCKS):
                 nc.tensor.transpose(bank[:, r, :], mask_bias[:, i, BANK + r * P : BANK + (r + 1) * P], ident_bf[:])
             mask_banks[i] = bank
@@ -114,12 +109,78 @@ def tile_dualmodehead_t_kernel(tc, q, k, v, mask, mode, out):
             operand[b] = {}
 
         def load_values(b):
-            v_raw = loads.tile([P, PASSES, PACK, DV], BF16, name="v_raw")
+            v_raw = loads.tile([P, PASSES, PACK, DV], BF16, name="v_raw", bufs=3)
             nc.sync.dma_start(
                 out=v_raw[:].rearrange("p g (u e) w -> p (g u) (e w)", e=2),
                 in_=v[b].rearrange("(c p e) w -> p c (e w)", p=P, e=2),
             )
             natural[b]["v"] = v_raw
+
+        def tick():
+            zero = small.tile([P, 1], F32, name="zero")
+            nc.vector.memset(zero[:], 0.0)
+            return zero[:, 0:1]
+
+        def blend_scale(b, zero):
+            k_nat = natural[b]["k"]
+            k_meson = loads.tile([P, TILES, D], F32, name="k_meson")
+            k_baryon = loads.tile([P, TILES, D], F32, name="k_baryon")
+            natural[b]["k_meson"] = k_meson
+            natural[b]["k_baryon"] = k_baryon
+            nc.gpsimd.tensor_scalar(
+                out=k_meson[:], in0=k_nat[:], scalar1=c_meson[:, 0:1], scalar2=zero, op0=ALU.mult, op1=ALU.add
+            )
+            nc.gpsimd.tensor_scalar(
+                out=k_baryon[:, :, 1:D], in0=k_nat[:, :, 0 : D - 1], scalar1=c_baryon[:, 0:1], scalar2=zero,
+                op0=ALU.mult, op1=ALU.add,
+            )
+            nc.gpsimd.tensor_scalar(
+                out=k_baryon[:, :, 0:1], in0=k_nat[:, :, D - 1 : D], scalar1=c_baryon[:, 0:1], scalar2=zero,
+                op0=ALU.mult, op1=ALU.add,
+            )
+
+        def blend_add(b):
+            k_meson = natural[b]["k_meson"]
+            nc.gpsimd.tensor_tensor(out=k_meson[:], in0=k_meson[:], in1=natural[b]["k_baryon"][:], op=ALU.add)
+
+        def blend_hi(b, zero):
+            k_parts = loads.tile([P, 2, TILES, D], BF16, name="k_parts")
+            natural[b]["k_parts"] = k_parts
+            nc.gpsimd.tensor_scalar(
+                out=k_parts[:, 0, :, :], in0=natural[b]["k_meson"][:], scalar1=1.0, scalar2=zero,
+                op0=ALU.mult, op1=ALU.add,
+            )
+
+        def blend_lo(b):
+            k_parts = natural[b]["k_parts"]
+            nc.gpsimd.tensor_tensor(
+                out=k_parts[:, 1, :, :], in0=natural[b]["k_meson"][:], in1=k_parts[:, 0, :, :], op=ALU.subtract
+            )
+
+        def group_quarter(b, quarter, zero):
+            if quarter == 0:
+                natural[b]["v_grouped"] = loads.tile(
+                    [P, PASSES, DV, PACK], BF16, name="v_grouped", align_bytes=64, bufs=3
+                )
+            g, half = divmod(quarter, 2)
+            columns = slice(half * (DV // 2), (half + 1) * (DV // 2))
+            nc.gpsimd.tensor_scalar(
+                out=natural[b]["v_grouped"][:, g, columns, :],
+                in0=natural[b]["v"][:, g, :, columns].rearrange("p t w -> p w t"),
+                scalar1=1.0, scalar2=zero, op0=ALU.mult, op1=ALU.add,
+            )
+
+        def prepare(b, piece):
+            zero = tick()
+            group_quarter(b, piece, zero)
+            if piece == 0:
+                blend_scale(b, zero)
+            elif piece == 1:
+                blend_add(b)
+            elif piece == 2:
+                blend_hi(b, zero)
+            else:
+                blend_lo(b)
 
         def blend_keys(b, engines):
             k_nat = natural[b]["k"]
@@ -150,15 +211,6 @@ def tile_dualmodehead_t_kernel(tc, q, k, v, mask, mode, out):
                     out=k_parts[:, 1, js, :], in0=k_meson[:, js, :], in1=k_parts[:, 0, js, :], op=ALU.subtract
                 )
             natural[b]["k_parts"] = k_parts
-
-        def group_values(b, engine):
-            v_grouped = loads.tile([P, PASSES, DV, PACK], BF16, name="v_grouped", align_bytes=64)
-            for g in range(PASSES):
-                engine.tensor_scalar(
-                    out=v_grouped[:, g, :, :], in0=natural[b]["v"][:, g, :, :].rearrange("p t w -> p w t"),
-                    scalar1=1.0, scalar2=0.0, op0=ALU.mult, op1=ALU.add,
-                )
-            natural[b]["v_grouped"] = v_grouped
 
         def turn_queries(b):
             bank = psum_t.tile([P, T], BF16, name="bank_q", tag="bank_t")
@@ -212,7 +264,7 @@ def tile_dualmodehead_t_kernel(tc, q, k, v, mask, mode, out):
             qT_tile = operand[b]["qT"][:, i * P : (i + 1) * P]
             live[n] = {"s": []}
             for h in range(HALVES):
-                s_bank = (psum_a, psum_b)[h].tile([P, BANK], F32, name="s_bank")
+                s_bank = (psum_a, psum_b)[h].tile([P, BANK], F32, name="s_bank", tag="s_bank")
                 nc.tensor.matmul(s_bank[:], lhsT=qT_tile, rhs=operand[b]["kT"][:, h, 0, :], start=True, stop=False)
                 nc.tensor.matmul(
                     s_bank[:], lhsT=qT_tile, rhs=operand[b]["kT"][:, h, 1, :], start=False,
@@ -347,18 +399,17 @@ def tile_dualmodehead_t_kernel(tc, q, k, v, mask, mode, out):
 
         load_batch(0)
         load_mask(0)
+        load_batch(1)
         load_mask(1)
         load_mask(2)
         load_values(0)
         load_mask(3)
-        load_batch(1)
         load_mask(4)
         load_values(1)
         load_mask(5)
         blend_keys(0, [nc.vector, nc.gpsimd])
-        group_values(0, nc.gpsimd)
-        blend_keys(1, [nc.gpsimd, nc.gpsimd])
-        group_values(1, nc.gpsimd)
+        blend_scale(1, 0.0)
+        blend_add(1)
         turn_queries(0)
         keep_queries(0)
         turn_keys(0, 0)
@@ -381,11 +432,9 @@ def tile_dualmodehead_t_kernel(tc, q, k, v, mask, mode, out):
 
         for t in range(N_TILES + 6):
             b, i = divmod(t, TILES)
-            if i == 4 and b + 2 < B:
+            if i == 0 and b + 2 < B:
                 load_batch(b + 2)
                 load_values(b + 2)
-                blend_keys(b + 2, [nc.gpsimd, nc.gpsimd])
-                group_values(b + 2, nc.gpsimd)
             if t + 6 < TILES:
                 load_mask(t + 6)
             on_group(product, t - 5)
@@ -399,27 +448,52 @@ def tile_dualmodehead_t_kernel(tc, q, k, v, mask, mode, out):
             on(add_mask, t + 1)
             on(row_max, t)
             on_group(quantise, t - 4)
-            on_group(invert_sums, t - 4)
+            if t == 4:
+                quantise_values(0)
+            if b + 1 < B and i == 6:
+                quantise_values(b + 1)
             if t + 2 < TILES:
                 convert_mask(t + 2)
+            if t == 0:
+                zero = tick()
+                blend_hi(1, zero)
+                group_quarter(0, 0, zero)
+                group_quarter(0, 1, zero)
+            if t == 1:
+                group_quarter(0, 2, tick())
+                blend_lo(1)
+            if t == 2:
+                zero = tick()
+                group_quarter(0, 3, zero)
+                group_quarter(1, 0, zero)
             if t == 3:
-                quantise_values(0)
+                zero = tick()
+                group_quarter(1, 1, zero)
+                group_quarter(1, 2, zero)
+                group_quarter(1, 3, zero)
+            if t == 4:
+                prepare(2, 0)
+            if t >= 5 and t % 2 == 1 and t < 8 * B - 14:
+                piece = (t - 3) // 2
+                prepare(2 + piece // 4, piece % 4)
+            on_group(invert_sums, t - 4)
+            if 1 <= t <= TILES:
+                keep_mask(t - 1)
             if b + 1 < B:
-                if i == 1:
-                    keep_queries(b + 1)
                 if i == 3:
+                    keep_queries(b + 1)
+                if i == 4:
                     keep_keys(b + 1, 0)
                 if i == 5:
                     keep_keys(b + 1, 1)
-                if i == 6:
-                    quantise_values(b + 1)
-            if 2 <= t < TILES + 2:
-                turn_mask(t - 2)
-                keep_mask(t - 2)
+            if t < 6:
+                turn_mask(t, psum_b, "s_bank")
+            elif t < TILES:
+                turn_mask(t, psum_t, "bank_t")
             if b + 1 < B:
-                if i == 0:
-                    turn_queries(b + 1)
                 if i == 2:
+                    turn_queries(b + 1)
+                if i == 3:
                     turn_keys(b + 1, 0)
                 if i == 4:
                     turn_keys(b + 1, 1)

@@ -23,6 +23,8 @@ BLOCKS = BANK // P
 PACK = 4
 K_PASS = P * PACK
 PASSES = T // K_PASS
+VECTOR_REGROUPS_FROM = N_TILES - 2
+VECTOR_FINISHES_FROM = N_TILES - 2
 FIRST_ON_TENSOR = 8
 GROUP = 2
 MASK_WORDS = 2
@@ -308,33 +310,32 @@ def tile_dualmodehead_t_kernel(tc, q, k, v, mask, mode, out):
             j, m = divmod(n, GROUP)
             if m == 0:
                 grouped[j] = {"row_sum": small.tile([P, GROUP], F32, name="row_sum")}
+                if on_tensor(n):
+                    grouped[j]["half_sums"] = small.tile([P, GROUP, HALVES], F32, name="half_sums")
             e = work.tile([P, T], BF16, name="e")
             row_sum = grouped[j]["row_sum"][:, m : m + 1]
             neg_max = live[n]["neg_max"][:, 0:1]
             if mask_on_tensor(n, 1):
-                half_sum = small.tile([P, HALVES], F32, name="half_sum")
+                half_sums = grouped[j]["half_sums"]
                 nc.scalar.activation(
                     out=e[:, BANK:T], in_=live[n]["s"][1][:], func=ACT.Exp, bias=neg_max, scale=1.0,
-                    accum_out=half_sum[:, 1:2],
+                    accum_out=half_sums[:, m, 1:2],
                 )
                 nc.scalar.activation(
                     out=e[:, 0:BANK], in_=live[n]["s_masked"][:, 0:BANK], func=ACT.Exp, bias=neg_max, scale=1.0,
-                    accum_out=half_sum[:, 0:1],
+                    accum_out=half_sums[:, m, 0:1],
                 )
-                live[n]["half_sum"] = half_sum
             else:
                 nc.scalar.activation(
                     out=e[:], in_=live[n]["s_masked"][:], func=ACT.Exp, bias=neg_max, scale=1.0, accum_out=row_sum
                 )
             live[n]["e"] = e
 
-        def add_half_sums(n):
-            if on_tensor(n):
-                j, m = divmod(n, GROUP)
-                half_sum = live[n]["half_sum"]
-                nc.scalar.activation(
-                    out=grouped[j]["row_sum"][:, m : m + 1], in_=half_sum[:, 0:1], func=ACT.Identity,
-                    bias=half_sum[:, 1:2], scale=1.0,
+        def add_half_sums(j):
+            if on_tensor(j * GROUP):
+                half_sums = grouped[j]["half_sums"]
+                nc.gpsimd.tensor_tensor(
+                    out=grouped[j]["row_sum"][:], in0=half_sums[:, :, 0], in1=half_sums[:, :, 1], op=ALU.add
                 )
 
         def invert_sums(j):
@@ -353,7 +354,8 @@ def tile_dualmodehead_t_kernel(tc, q, k, v, mask, mode, out):
             j, m = divmod(n, GROUP)
             if m == 0:
                 grouped[j]["e"] = work.tile([P, GROUP, PASSES * P * PACK], BF16, name="e_grouped", align_bytes=64)
-            nc.scalar.copy(
+            copy = nc.vector.tensor_copy if n >= VECTOR_REGROUPS_FROM else nc.scalar.copy
+            copy(
                 out=grouped[j]["e"][:, m, :].bitcast(F32).rearrange("p (g q u) -> p g q u", g=PASSES, u=2),
                 in_=live[n]["eT_bank"][:].rearrange("p (g u) q -> p g q u", u=2),
             )
@@ -389,10 +391,13 @@ def tile_dualmodehead_t_kernel(tc, q, k, v, mask, mode, out):
             b, i = divmod(j * GROUP, TILES)
             o_sb = work.tile([P, GROUP, DV], F32, name="o_sb")
             for m in range(GROUP):
-                nc.scalar.activation(
-                    out=o_sb[:, m, :], in_=grouped[j]["o_bank"][:, m, :], func=ACT.Copy,
-                    scale=grouped[j]["inv_sum"][:, m : m + 1],
-                )
+                inv_sum = grouped[j]["inv_sum"][:, m : m + 1]
+                if m == 1 and j * GROUP >= VECTOR_FINISHES_FROM:
+                    nc.vector.tensor_scalar_mul(out=o_sb[:, m, :], in0=grouped[j]["o_bank"][:, m, :], scalar1=inv_sum)
+                else:
+                    nc.scalar.activation(
+                        out=o_sb[:, m, :], in_=grouped[j]["o_bank"][:, m, :], func=ACT.Copy, scale=inv_sum
+                    )
             nc.sync.dma_start(
                 out=out[b, i * P : (i + GROUP) * P, :].rearrange("(m p) w -> p m w", p=P), in_=o_sb[:]
             )
@@ -441,16 +446,15 @@ def tile_dualmodehead_t_kernel(tc, q, k, v, mask, mode, out):
             on(exponent, t - 1)
             on(scores, t + 2)
             on(regroup, t - 3)
-            on(add_half_sums, t - 1)
             on(turn, t - 2)
             on_group(finish, t - 5)
             on(fold, t)
             on(add_mask, t + 1)
             on(row_max, t)
             on_group(quantise, t - 4)
-            if t == 4:
+            if t == 5:
                 quantise_values(0)
-            if b + 1 < B and i == 6:
+            if b + 1 < B and i == 7:
                 quantise_values(b + 1)
             if t + 2 < TILES:
                 convert_mask(t + 2)
@@ -471,6 +475,7 @@ def tile_dualmodehead_t_kernel(tc, q, k, v, mask, mode, out):
                 group_quarter(1, 1, zero)
                 group_quarter(1, 2, zero)
                 group_quarter(1, 3, zero)
+            on_group(add_half_sums, t - 1)
             if t == 4:
                 prepare(2, 0)
             if t >= 5 and t % 2 == 1 and t < 8 * B - 14:
@@ -480,9 +485,9 @@ def tile_dualmodehead_t_kernel(tc, q, k, v, mask, mode, out):
             if 1 <= t <= TILES:
                 keep_mask(t - 1)
             if b + 1 < B:
-                if i == 3:
+                if i == 1:
                     keep_queries(b + 1)
-                if i == 4:
+                if i == 3:
                     keep_keys(b + 1, 0)
                 if i == 5:
                     keep_keys(b + 1, 1)
@@ -491,9 +496,9 @@ def tile_dualmodehead_t_kernel(tc, q, k, v, mask, mode, out):
             elif t < TILES:
                 turn_mask(t, psum_t, "bank_t")
             if b + 1 < B:
-                if i == 2:
+                if i == 0:
                     turn_queries(b + 1)
-                if i == 3:
+                if i == 2:
                     turn_keys(b + 1, 0)
                 if i == 4:
                     turn_keys(b + 1, 1)

@@ -23,9 +23,11 @@ BLOCKS = BANK // P
 PACK = 4
 K_PASS = P * PACK
 PASSES = T // K_PASS
-VECTOR_REGROUPS_FROM = N_TILES - 2
+VECTOR_REGROUPS_FROM = N_TILES - 3
 VECTOR_FINISHES_FROM = N_TILES - 2
-FIRST_ON_TENSOR = 8
+FIRST_ON_TENSOR = 4
+MASK_STEPS = (1, 3, 5, 6, 7)
+TURNED = 5
 GROUP = 2
 MASK_WORDS = 2
 MASKED = -(2.0**100)
@@ -71,7 +73,7 @@ def tile_dualmodehead_t_kernel(tc, q, k, v, mask, mode, out):
 
         mask_bias = const.tile([P, TILES, T], BF16)
 
-        mask_turned = const.tile([P, TILES, BLOCKS, P], F32)
+        mask_turned = const.tile([P, TURNED, BLOCKS, P], F32)
 
         mask_raw = {}
 
@@ -102,13 +104,16 @@ def tile_dualmodehead_t_kernel(tc, q, k, v, mask, mode, out):
         natural = {}
         operand = {}
 
-        def load_batch(b):
+        def load_keys(b):
             k_nat = loads.tile([P, TILES, D], BF16, name="k_nat")
             nc.sync.dma_start(out=k_nat[:], in_=k[b].rearrange("(j p) d -> p j d", p=P))
+            natural[b] = {"k": k_nat}
+            operand[b] = {}
+
+        def load_queries(b):
             q_nat = loads.tile([P, TILES, D], BF16, name="q_nat")
             nc.sync.dma_start(out=q_nat[:], in_=q[b].rearrange("(j p) d -> p j d", p=P))
-            natural[b] = {"k": k_nat, "q": q_nat}
-            operand[b] = {}
+            natural[b]["q"] = q_nat
 
         def load_values(b):
             v_raw = loads.tile([P, PASSES, PACK, DV], BF16, name="v_raw", bufs=3)
@@ -118,26 +123,25 @@ def tile_dualmodehead_t_kernel(tc, q, k, v, mask, mode, out):
             )
             natural[b]["v"] = v_raw
 
-        def tick():
-            zero = small.tile([P, 1], F32, name="zero")
-            nc.vector.memset(zero[:], 0.0)
-            return zero[:, 0:1]
+        def gate(column):
+            passed = small.tile([P, 1], column.dtype, name="passed")
+            nc.gpsimd.tensor_copy(out=passed[:], in_=column)
 
-        def blend_scale(b, zero):
+        def blend_scale(b):
             k_nat = natural[b]["k"]
             k_meson = loads.tile([P, TILES, D], F32, name="k_meson")
             k_baryon = loads.tile([P, TILES, D], F32, name="k_baryon")
             natural[b]["k_meson"] = k_meson
             natural[b]["k_baryon"] = k_baryon
             nc.gpsimd.tensor_scalar(
-                out=k_meson[:], in0=k_nat[:], scalar1=c_meson[:, 0:1], scalar2=zero, op0=ALU.mult, op1=ALU.add
+                out=k_meson[:], in0=k_nat[:], scalar1=c_meson[:, 0:1], scalar2=0.0, op0=ALU.mult, op1=ALU.add
             )
             nc.gpsimd.tensor_scalar(
-                out=k_baryon[:, :, 1:D], in0=k_nat[:, :, 0 : D - 1], scalar1=c_baryon[:, 0:1], scalar2=zero,
+                out=k_baryon[:, :, 1:D], in0=k_nat[:, :, 0 : D - 1], scalar1=c_baryon[:, 0:1], scalar2=0.0,
                 op0=ALU.mult, op1=ALU.add,
             )
             nc.gpsimd.tensor_scalar(
-                out=k_baryon[:, :, 0:1], in0=k_nat[:, :, D - 1 : D], scalar1=c_baryon[:, 0:1], scalar2=zero,
+                out=k_baryon[:, :, 0:1], in0=k_nat[:, :, D - 1 : D], scalar1=c_baryon[:, 0:1], scalar2=0.0,
                 op0=ALU.mult, op1=ALU.add,
             )
 
@@ -145,11 +149,11 @@ def tile_dualmodehead_t_kernel(tc, q, k, v, mask, mode, out):
             k_meson = natural[b]["k_meson"]
             nc.gpsimd.tensor_tensor(out=k_meson[:], in0=k_meson[:], in1=natural[b]["k_baryon"][:], op=ALU.add)
 
-        def blend_hi(b, zero):
+        def blend_hi(b):
             k_parts = loads.tile([P, 2, TILES, D], BF16, name="k_parts")
             natural[b]["k_parts"] = k_parts
             nc.gpsimd.tensor_scalar(
-                out=k_parts[:, 0, :, :], in0=natural[b]["k_meson"][:], scalar1=1.0, scalar2=zero,
+                out=k_parts[:, 0, :, :], in0=natural[b]["k_meson"][:], scalar1=1.0, scalar2=0.0,
                 op0=ALU.mult, op1=ALU.add,
             )
 
@@ -159,7 +163,7 @@ def tile_dualmodehead_t_kernel(tc, q, k, v, mask, mode, out):
                 out=k_parts[:, 1, :, :], in0=natural[b]["k_meson"][:], in1=k_parts[:, 0, :, :], op=ALU.subtract
             )
 
-        def group_quarter(b, quarter, zero):
+        def group_quarter(b, quarter):
             if quarter == 0:
                 natural[b]["v_grouped"] = loads.tile(
                     [P, PASSES, DV, PACK], BF16, name="v_grouped", align_bytes=64, bufs=3
@@ -169,18 +173,17 @@ def tile_dualmodehead_t_kernel(tc, q, k, v, mask, mode, out):
             nc.gpsimd.tensor_scalar(
                 out=natural[b]["v_grouped"][:, g, columns, :],
                 in0=natural[b]["v"][:, g, :, columns].rearrange("p t w -> p w t"),
-                scalar1=1.0, scalar2=zero, op0=ALU.mult, op1=ALU.add,
+                scalar1=1.0, scalar2=0.0, op0=ALU.mult, op1=ALU.add,
             )
 
         def prepare(b, piece):
-            zero = tick()
-            group_quarter(b, piece, zero)
+            group_quarter(b, piece)
             if piece == 0:
-                blend_scale(b, zero)
+                blend_scale(b)
             elif piece == 1:
                 blend_add(b)
             elif piece == 2:
-                blend_hi(b, zero)
+                blend_hi(b)
             else:
                 blend_lo(b)
 
@@ -272,7 +275,11 @@ def tile_dualmodehead_t_kernel(tc, q, k, v, mask, mode, out):
                     s_bank[:], lhsT=qT_tile, rhs=operand[b]["kT"][:, h, 1, :], start=False,
                     stop=not mask_on_tensor(n, h),
                 )
-                if mask_on_tensor(n, h):
+                if mask_on_tensor(n, h) and (b == 0 or i >= TURNED):
+                    nc.tensor.matmul(
+                        s_bank[:], lhsT=ident_bf[:], rhs=mask_bias[:, i, BANK:T], start=False, stop=True
+                    )
+                elif mask_on_tensor(n, h):
                     for r in range(BLOCKS):
                         nc.tensor.matmul(
                             s_bank[:, r * P : (r + 1) * P], lhsT=mask_turned[:, i, r, :], rhs=ident_f32[:],
@@ -392,7 +399,7 @@ def tile_dualmodehead_t_kernel(tc, q, k, v, mask, mode, out):
             o_sb = work.tile([P, GROUP, DV], F32, name="o_sb")
             for m in range(GROUP):
                 inv_sum = grouped[j]["inv_sum"][:, m : m + 1]
-                if m == 1 and j * GROUP >= VECTOR_FINISHES_FROM:
+                if m == 1 and (j % 2 == 1 or j * GROUP >= VECTOR_FINISHES_FROM):
                     nc.vector.tensor_scalar_mul(out=o_sb[:, m, :], in0=grouped[j]["o_bank"][:, m, :], scalar1=inv_sum)
                 else:
                     nc.scalar.activation(
@@ -402,10 +409,12 @@ def tile_dualmodehead_t_kernel(tc, q, k, v, mask, mode, out):
                 out=out[b, i * P : (i + GROUP) * P, :].rearrange("(m p) w -> p m w", p=P), in_=o_sb[:]
             )
 
-        load_batch(0)
+        load_keys(0)
+        load_queries(0)
         load_mask(0)
-        load_batch(1)
         load_mask(1)
+        load_keys(1)
+        load_queries(1)
         load_mask(2)
         load_values(0)
         load_mask(3)
@@ -413,8 +422,7 @@ def tile_dualmodehead_t_kernel(tc, q, k, v, mask, mode, out):
         load_values(1)
         load_mask(5)
         blend_keys(0, [nc.vector, nc.gpsimd])
-        blend_scale(1, 0.0)
-        blend_add(1)
+        blend_scale(1)
         turn_queries(0)
         keep_queries(0)
         turn_keys(0, 0)
@@ -422,10 +430,12 @@ def tile_dualmodehead_t_kernel(tc, q, k, v, mask, mode, out):
         convert_mask(0)
         turn_keys(0, 1)
         keep_keys(0, 1)
-        convert_mask(1)
         scores(0)
         scores(1)
         add_mask(0)
+        convert_mask(1)
+        gate(mask_bias[:, 1, 0:1])
+        blend_add(1)
 
         def on(stage, n):
             if 0 <= n < N_TILES:
@@ -438,7 +448,8 @@ def tile_dualmodehead_t_kernel(tc, q, k, v, mask, mode, out):
         for t in range(N_TILES + 6):
             b, i = divmod(t, TILES)
             if i == 0 and b + 2 < B:
-                load_batch(b + 2)
+                load_keys(b + 2)
+                load_queries(b + 2)
                 load_values(b + 2)
             if t + 6 < TILES:
                 load_mask(t + 6)
@@ -447,7 +458,6 @@ def tile_dualmodehead_t_kernel(tc, q, k, v, mask, mode, out):
             on(scores, t + 2)
             on(regroup, t - 3)
             on(turn, t - 2)
-            on_group(finish, t - 5)
             on(fold, t)
             on(add_mask, t + 1)
             on(row_max, t)
@@ -456,34 +466,38 @@ def tile_dualmodehead_t_kernel(tc, q, k, v, mask, mode, out):
                 quantise_values(0)
             if b + 1 < B and i == 7:
                 quantise_values(b + 1)
-            if t + 2 < TILES:
-                convert_mask(t + 2)
             if t == 0:
-                zero = tick()
-                blend_hi(1, zero)
-                group_quarter(0, 0, zero)
-                group_quarter(0, 1, zero)
+                convert_mask(2)
+            if 0 <= t < 5:
+                convert_mask(t + 3)
+            on_group(finish, t - 5)
+            on_group(add_half_sums, t - 1)
+            if t == 0:
+                gate(mask_bias[:, t + 3, 0:1])
+                blend_hi(1)
+                group_quarter(0, 0)
+                group_quarter(0, 1)
             if t == 1:
-                group_quarter(0, 2, tick())
+                gate(mask_bias[:, t + 3, 0:1])
+                group_quarter(0, 2)
                 blend_lo(1)
             if t == 2:
-                zero = tick()
-                group_quarter(0, 3, zero)
-                group_quarter(1, 0, zero)
+                gate(mask_bias[:, t + 3, 0:1])
+                group_quarter(0, 3)
+                group_quarter(1, 0)
             if t == 3:
-                zero = tick()
-                group_quarter(1, 1, zero)
-                group_quarter(1, 2, zero)
-                group_quarter(1, 3, zero)
-            on_group(add_half_sums, t - 1)
+                gate(mask_bias[:, t + 3, 0:1])
+                group_quarter(1, 1)
+                group_quarter(1, 2)
+                group_quarter(1, 3)
             if t == 4:
+                gate(mask_bias[:, t + 3, 0:1])
                 prepare(2, 0)
             if t >= 5 and t % 2 == 1 and t < 8 * B - 14:
                 piece = (t - 3) // 2
+                gate(grouped[(t - 4) // GROUP]["codes"][:, 0, 0, 0:1])
                 prepare(2 + piece // 4, piece % 4)
             on_group(invert_sums, t - 4)
-            if 1 <= t <= TILES:
-                keep_mask(t - 1)
             if b + 1 < B:
                 if i == 1:
                     keep_queries(b + 1)
@@ -491,10 +505,8 @@ def tile_dualmodehead_t_kernel(tc, q, k, v, mask, mode, out):
                     keep_keys(b + 1, 0)
                 if i == 5:
                     keep_keys(b + 1, 1)
-            if t < 6:
-                turn_mask(t, psum_b, "s_bank")
-            elif t < TILES:
-                turn_mask(t, psum_t, "bank_t")
+            if t in (2, 4, 6, 7, 8):
+                keep_mask(MASK_STEPS.index(t - 1))
             if b + 1 < B:
                 if i == 0:
                     turn_queries(b + 1)
@@ -502,3 +514,5 @@ def tile_dualmodehead_t_kernel(tc, q, k, v, mask, mode, out):
                     turn_keys(b + 1, 0)
                 if i == 4:
                     turn_keys(b + 1, 1)
+            if t in MASK_STEPS:
+                turn_mask(MASK_STEPS.index(t), psum_t, "bank_t")

@@ -26,7 +26,7 @@ PASSES = T // K_PASS
 VECTOR_REGROUPS_FROM = N_TILES - 3
 VECTOR_FINISHES_FROM = N_TILES - 2
 FIRST_ON_TENSOR = 4
-MASK_STEPS = (1, 3, 5, 6, 7)
+MASK_STEPS = (0, 2, 5, 6, 7)
 TURNED = 5
 GROUP = 2
 MASK_WORDS = 2
@@ -48,9 +48,7 @@ def tile_dualmodehead_t_kernel(tc, q, k, v, mask, mode, out):
         small = ctx.enter_context(tc.tile_pool(name="small", bufs=8))
         psum_a = ctx.enter_context(tc.psum_pool(name="psum_a", bufs=2))
         psum_b = ctx.enter_context(tc.psum_pool(name="psum_b", bufs=3))
-        psum_t = ctx.enter_context(tc.psum_pool(name="psum_t", bufs=1))
-        psum_e = ctx.enter_context(tc.psum_pool(name="psum_e", bufs=1))
-        psum_o = ctx.enter_context(tc.psum_pool(name="psum_o", bufs=1))
+        psum_t = ctx.enter_context(tc.psum_pool(name="psum_t", bufs=3))
         ctx.enter_context(tc.manual_schedule())
 
         ident_bf = const.tile([P, P], BF16)
@@ -187,35 +185,30 @@ def tile_dualmodehead_t_kernel(tc, q, k, v, mask, mode, out):
             else:
                 blend_lo(b)
 
-        def blend_keys(b, engines):
-            k_nat = natural[b]["k"]
+        def blend_first_keys():
+            k_nat = natural[0]["k"]
             k_meson = loads.tile([P, TILES, D], F32, name="k_meson")
             k_baryon = loads.tile([P, TILES, D], F32, name="k_baryon")
             k_parts = loads.tile([P, 2, TILES, D], BF16, name="k_parts")
-            for h in range(HALVES):
-                engine = engines[h]
-                js = slice(h * BLOCKS, (h + 1) * BLOCKS)
-                engine.tensor_scalar(
-                    out=k_meson[:, js, :], in0=k_nat[:, js, :], scalar1=c_meson[:, 0:1], scalar2=0.0,
-                    op0=ALU.mult, op1=ALU.add,
+            natural[0]["k_parts"] = k_parts
+            halves = [slice(h * BLOCKS, (h + 1) * BLOCKS) for h in range(HALVES)]
+            for js in halves:
+                nc.vector.tensor_scalar_mul(out=k_meson[:, js, :], in0=k_nat[:, js, :], scalar1=c_meson[:, 0:1])
+            for js in halves:
+                nc.vector.scalar_tensor_tensor(
+                    out=k_baryon[:, js, 1:D], in0=k_nat[:, js, 0 : D - 1], scalar=c_baryon[:, 0:1],
+                    in1=k_meson[:, js, 1:D], op0=ALU.mult, op1=ALU.add,
                 )
-                engine.tensor_scalar(
-                    out=k_baryon[:, js, 1:D], in0=k_nat[:, js, 0 : D - 1], scalar1=c_baryon[:, 0:1],
-                    scalar2=0.0, op0=ALU.mult, op1=ALU.add,
+                nc.vector.scalar_tensor_tensor(
+                    out=k_baryon[:, js, 0:1], in0=k_nat[:, js, D - 1 : D], scalar=c_baryon[:, 0:1],
+                    in1=k_meson[:, js, 0:1], op0=ALU.mult, op1=ALU.add,
                 )
-                engine.tensor_scalar(
-                    out=k_baryon[:, js, 0:1], in0=k_nat[:, js, D - 1 : D], scalar1=c_baryon[:, 0:1],
-                    scalar2=0.0, op0=ALU.mult, op1=ALU.add,
+            for js in halves:
+                nc.vector.tensor_copy(out=k_parts[:, 0, js, :], in_=k_baryon[:, js, :])
+            for js in halves:
+                nc.vector.tensor_tensor(
+                    out=k_parts[:, 1, js, :], in0=k_baryon[:, js, :], in1=k_parts[:, 0, js, :], op=ALU.subtract
                 )
-                engine.tensor_tensor(out=k_meson[:, js, :], in0=k_meson[:, js, :], in1=k_baryon[:, js, :], op=ALU.add)
-                engine.tensor_scalar(
-                    out=k_parts[:, 0, js, :], in0=k_meson[:, js, :], scalar1=1.0, scalar2=0.0,
-                    op0=ALU.mult, op1=ALU.add,
-                )
-                engine.tensor_tensor(
-                    out=k_parts[:, 1, js, :], in0=k_meson[:, js, :], in1=k_parts[:, 0, js, :], op=ALU.subtract
-                )
-            natural[b]["k_parts"] = k_parts
 
         def turn_queries(b):
             bank = psum_t.tile([P, T], BF16, name="bank_q", tag="bank_t")
@@ -239,8 +232,8 @@ def tile_dualmodehead_t_kernel(tc, q, k, v, mask, mode, out):
                     )
             operand[b]["bank_k"] = bank
 
-        def keep_keys(b, h):
-            nc.scalar.copy(
+        def keep_keys(b, h, copy):
+            copy(
                 out=operand[b]["kT"][:, h, :, :], in_=operand[b]["bank_k"][:].rearrange("p a r c -> p a (r c)")
             )
 
@@ -352,7 +345,7 @@ def tile_dualmodehead_t_kernel(tc, q, k, v, mask, mode, out):
 
         def turn(n):
             e_words = live[n]["e"][:].bitcast(F32)
-            eT_bank = psum_e.tile([P, PASSES * 2, P], F32, name="eT_bank")
+            eT_bank = psum_t.tile([P, PASSES * 2, P], F32, name="eT_bank", tag="bank_t")
             for c in range(PASSES * 2):
                 nc.tensor.transpose(eT_bank[:, c, :], e_words[:, c * P : (c + 1) * P], ident_f32[:])
             live[n]["eT_bank"] = eT_bank
@@ -380,7 +373,7 @@ def tile_dualmodehead_t_kernel(tc, q, k, v, mask, mode, out):
 
         def product(j):
             ops = operand[(j * GROUP) // TILES]
-            o_bank = psum_o.tile([P, GROUP, DV], F32, name="o_bank")
+            o_bank = psum_t.tile([P, GROUP, DV], F32, name="o_bank", tag="bank_t")
             for m in range(GROUP):
                 for g in range(PASSES):
                     nc.tensor.matmul_mx(
@@ -397,13 +390,16 @@ def tile_dualmodehead_t_kernel(tc, q, k, v, mask, mode, out):
         def finish(j):
             b, i = divmod(j * GROUP, TILES)
             o_sb = work.tile([P, GROUP, DV], F32, name="o_sb")
-            for m in range(GROUP):
-                inv_sum = grouped[j]["inv_sum"][:, m : m + 1]
-                if m == 1 and (j % 2 == 1 or j * GROUP >= VECTOR_FINISHES_FROM):
-                    nc.vector.tensor_scalar_mul(out=o_sb[:, m, :], in0=grouped[j]["o_bank"][:, m, :], scalar1=inv_sum)
-                else:
+            if j % 4 == 3:
+                nc.vector.tensor_tensor(
+                    out=o_sb[:], in0=grouped[j]["o_bank"][:],
+                    in1=grouped[j]["inv_sum"][:].unsqueeze(2).to_broadcast([P, GROUP, DV]), op=ALU.mult,
+                )
+            else:
+                for m in range(GROUP):
                     nc.scalar.activation(
-                        out=o_sb[:, m, :], in_=grouped[j]["o_bank"][:, m, :], func=ACT.Copy, scale=inv_sum
+                        out=o_sb[:, m, :], in_=grouped[j]["o_bank"][:, m, :], func=ACT.Copy,
+                        scale=grouped[j]["inv_sum"][:, m : m + 1],
                     )
             nc.sync.dma_start(
                 out=out[b, i * P : (i + GROUP) * P, :].rearrange("(m p) w -> p m w", p=P), in_=o_sb[:]
@@ -414,28 +410,27 @@ def tile_dualmodehead_t_kernel(tc, q, k, v, mask, mode, out):
         load_mask(0)
         load_mask(1)
         load_keys(1)
-        load_queries(1)
         load_mask(2)
-        load_values(0)
+        load_queries(1)
         load_mask(3)
+        load_values(0)
         load_mask(4)
-        load_values(1)
         load_mask(5)
-        blend_keys(0, [nc.vector, nc.gpsimd])
-        blend_scale(1)
+        load_values(1)
+        blend_first_keys()
         turn_queries(0)
         keep_queries(0)
         turn_keys(0, 0)
-        keep_keys(0, 0)
+        keep_keys(0, 0, nc.scalar.copy)
         convert_mask(0)
         turn_keys(0, 1)
-        keep_keys(0, 1)
+        keep_keys(0, 1, nc.vector.tensor_copy)
+        convert_mask(1)
+        gate(mask_bias[:, 1, 0:1])
+        blend_scale(1)
         scores(0)
         scores(1)
         add_mask(0)
-        convert_mask(1)
-        gate(mask_bias[:, 1, 0:1])
-        blend_add(1)
 
         def on(stage, n):
             if 0 <= n < N_TILES:
@@ -447,7 +442,7 @@ def tile_dualmodehead_t_kernel(tc, q, k, v, mask, mode, out):
 
         for t in range(N_TILES + 6):
             b, i = divmod(t, TILES)
-            if i == 0 and b + 2 < B:
+            if i == (3 if b == 0 else 0) and b + 2 < B:
                 load_keys(b + 2)
                 load_queries(b + 2)
                 load_values(b + 2)
@@ -474,43 +469,45 @@ def tile_dualmodehead_t_kernel(tc, q, k, v, mask, mode, out):
             on_group(add_half_sums, t - 1)
             if t == 0:
                 gate(mask_bias[:, t + 3, 0:1])
-                blend_hi(1)
-                group_quarter(0, 0)
-                group_quarter(0, 1)
+                blend_add(1)
             if t == 1:
                 gate(mask_bias[:, t + 3, 0:1])
-                group_quarter(0, 2)
-                blend_lo(1)
+                group_quarter(0, 0)
+                blend_hi(1)
             if t == 2:
                 gate(mask_bias[:, t + 3, 0:1])
-                group_quarter(0, 3)
-                group_quarter(1, 0)
+                blend_lo(1)
             if t == 3:
                 gate(mask_bias[:, t + 3, 0:1])
-                group_quarter(1, 1)
-                group_quarter(1, 2)
-                group_quarter(1, 3)
+                for quarter in (1, 2, 3):
+                    group_quarter(0, quarter)
             if t == 4:
                 gate(mask_bias[:, t + 3, 0:1])
-                prepare(2, 0)
+                for quarter in range(4):
+                    group_quarter(1, quarter)
             if t >= 5 and t % 2 == 1 and t < 8 * B - 14:
-                piece = (t - 3) // 2
                 gate(grouped[(t - 4) // GROUP]["codes"][:, 0, 0, 0:1])
-                prepare(2 + piece // 4, piece % 4)
+                if t < TILES:
+                    prepare(2, (t - 5) // 2)
+                elif t == 9:
+                    prepare(2, 2)
+                    prepare(2, 3)
+                else:
+                    prepare(3 + (t - 11) // TILES, (t - 11) % TILES // 2)
             on_group(invert_sums, t - 4)
             if b + 1 < B:
-                if i == 1:
+                if i == 2:
                     keep_queries(b + 1)
-                if i == 3:
-                    keep_keys(b + 1, 0)
+                if i == 4:
+                    keep_keys(b + 1, 0, nc.scalar.copy)
                 if i == 5:
-                    keep_keys(b + 1, 1)
-            if t in (2, 4, 6, 7, 8):
+                    keep_keys(b + 1, 1, nc.scalar.copy)
+            if t in (1, 3, 6, 7, 8):
                 keep_mask(MASK_STEPS.index(t - 1))
             if b + 1 < B:
-                if i == 0:
+                if i == 1:
                     turn_queries(b + 1)
-                if i == 2:
+                if i == 3:
                     turn_keys(b + 1, 0)
                 if i == 4:
                     turn_keys(b + 1, 1)

@@ -25,9 +25,11 @@ K_PASS = P * PACK
 PASSES = T // K_PASS
 VECTOR_REGROUPS_FROM = N_TILES - 3
 VECTOR_FINISHES_FROM = N_TILES - 2
-FIRST_ON_TENSOR = 4
+FIRST_ON_TENSOR = 5
 MASK_STEPS = (0, 2, 5, 6, 7)
 TURNED = 5
+MASKS_ON_SCALAR = 4
+QUAD = 4
 GROUP = 2
 MASK_WORDS = 2
 MASKED = -(2.0**100)
@@ -82,6 +84,12 @@ def tile_dualmodehead_t_kernel(tc, q, k, v, mask, mode, out):
             )
 
         def convert_mask(i):
+            if i < MASKS_ON_SCALAR:
+                nc.scalar.activation(
+                    out=mask_bias[:, i, :], in_=mask_raw[i][:].bitcast(U32)[:, :, 0], func=ACT.Copy,
+                    scale=-MASKED, bias=MASKED,
+                )
+                return
             nc.vector.tensor_scalar(
                 out=mask_bias[:, i, :], in0=mask_raw[i][:, :, 0], scalar1=-MASKED, scalar2=MASKED, op0=ALU.mult, op1=ALU.add
             )
@@ -249,6 +257,7 @@ def tile_dualmodehead_t_kernel(tc, q, k, v, mask, mode, out):
             operand[b]["v_scales"] = v_scales
 
         live = {}
+        quads = {}
         grouped = {}
 
         def on_tensor(n):
@@ -309,21 +318,24 @@ def tile_dualmodehead_t_kernel(tc, q, k, v, mask, mode, out):
         def exponent(n):
             j, m = divmod(n, GROUP)
             if m == 0:
-                grouped[j] = {"row_sum": small.tile([P, GROUP], F32, name="row_sum")}
-                if on_tensor(n):
-                    grouped[j]["half_sums"] = small.tile([P, GROUP, HALVES], F32, name="half_sums")
+                grouped[j] = {}
+            c, r = divmod(n, QUAD)
+            if r == 0:
+                quads[c] = {"row_sum": small.tile([P, QUAD], F32, name="row_sum")}
+                if on_tensor(n + QUAD - 1):
+                    quads[c]["half_sums"] = small.tile([P, QUAD, HALVES], F32, name="half_sums")
             e = work.tile([P, T], BF16, name="e")
-            row_sum = grouped[j]["row_sum"][:, m : m + 1]
+            row_sum = quads[c]["row_sum"][:, r : r + 1]
             neg_max = live[n]["neg_max"][:, 0:1]
             if mask_on_tensor(n, 1):
-                half_sums = grouped[j]["half_sums"]
+                half_sums = quads[c]["half_sums"]
                 nc.scalar.activation(
                     out=e[:, BANK:T], in_=live[n]["s"][1][:], func=ACT.Exp, bias=neg_max, scale=1.0,
-                    accum_out=half_sums[:, m, 1:2],
+                    accum_out=half_sums[:, r, 1:2],
                 )
                 nc.scalar.activation(
                     out=e[:, 0:BANK], in_=live[n]["s_masked"][:, 0:BANK], func=ACT.Exp, bias=neg_max, scale=1.0,
-                    accum_out=half_sums[:, m, 0:1],
+                    accum_out=half_sums[:, r, 0:1],
                 )
             else:
                 nc.scalar.activation(
@@ -331,17 +343,19 @@ def tile_dualmodehead_t_kernel(tc, q, k, v, mask, mode, out):
                 )
             live[n]["e"] = e
 
-        def add_half_sums(j):
-            if on_tensor(j * GROUP):
-                half_sums = grouped[j]["half_sums"]
+        def add_half_sums(c):
+            halved = [r for r in range(QUAD) if on_tensor(c * QUAD + r)]
+            if halved:
+                half_sums = quads[c]["half_sums"]
+                rs = slice(halved[0], QUAD)
                 nc.gpsimd.tensor_tensor(
-                    out=grouped[j]["row_sum"][:], in0=half_sums[:, :, 0], in1=half_sums[:, :, 1], op=ALU.add
+                    out=quads[c]["row_sum"][:, rs], in0=half_sums[:, rs, 0], in1=half_sums[:, rs, 1], op=ALU.add
                 )
 
-        def invert_sums(j):
-            inv_sum = small.tile([P, GROUP], F32, name="inv_sum")
-            nc.vector.reciprocal(out=inv_sum[:], in_=grouped[j]["row_sum"][:])
-            grouped[j]["inv_sum"] = inv_sum
+        def invert_sums(c):
+            inv_sum = small.tile([P, QUAD], F32, name="inv_sum")
+            nc.vector.reciprocal(out=inv_sum[:], in_=quads[c]["row_sum"][:])
+            quads[c]["inv_sum"] = inv_sum
 
         def turn(n):
             e_words = live[n]["e"][:].bitcast(F32)
@@ -360,24 +374,24 @@ def tile_dualmodehead_t_kernel(tc, q, k, v, mask, mode, out):
                 in_=live[n]["eT_bank"][:].rearrange("p (g u) q -> p g q u", u=2),
             )
 
-        def quantise(j):
-            e_codes = work.tile([P, GROUP, PASSES, P], U32, name="e_codes", align_bytes=64)
-            e_scales = work.tile([P, GROUP, PASSES, P], U8, name="e_scales", align_bytes=64)
+        def quantise(j, members):
+            if members.start == 0:
+                grouped[j]["codes"] = work.tile([P, GROUP, PASSES, P], U32, name="e_codes", align_bytes=64)
+                grouped[j]["scales"] = work.tile([P, GROUP, PASSES, P], U8, name="e_scales", align_bytes=64)
             nc.vector.quantize_mx(
-                out=e_codes[:].rearrange("p m g q -> p (m g q)").bitcast(FP8X4),
-                scales=e_scales[:].rearrange("p m g q -> p (m g q)"),
-                in_=grouped[j]["e"][:].rearrange("p m c -> p (m c)"),
+                out=grouped[j]["codes"][:, members, :, :].rearrange("p m g q -> p (m g q)").bitcast(FP8X4),
+                scales=grouped[j]["scales"][:, members, :, :].rearrange("p m g q -> p (m g q)"),
+                in_=grouped[j]["e"][:, members, :].rearrange("p m c -> p (m c)"),
             )
-            grouped[j]["codes"] = e_codes
-            grouped[j]["scales"] = e_scales
 
-        def product(j):
+        def product(j, members):
             ops = operand[(j * GROUP) // TILES]
-            o_bank = psum_t.tile([P, GROUP, DV], F32, name="o_bank", tag="bank_t")
-            for m in range(GROUP):
+            if members.start == 0:
+                grouped[j]["o_bank"] = psum_t.tile([P, GROUP, DV], F32, name="o_bank", tag="bank_t")
+            for m in range(members.start, members.stop):
                 for g in range(PASSES):
                     nc.tensor.matmul_mx(
-                        out=o_bank[:, m, :],
+                        out=grouped[j]["o_bank"][:, m, :],
                         lhsT=grouped[j]["codes"][:, m, g, :].bitcast(FP8X4),
                         lhsT_scale=grouped[j]["scales"][:, m, g, :],
                         rhs=ops["v_codes"][:, g * DV : (g + 1) * DV].bitcast(FP8X4),
@@ -385,24 +399,30 @@ def tile_dualmodehead_t_kernel(tc, q, k, v, mask, mode, out):
                         start=(g == 0),
                         stop=(g == PASSES - 1),
                     )
-            grouped[j]["o_bank"] = o_bank
 
-        def finish(j):
+        def finish(j, members, on_vector):
             b, i = divmod(j * GROUP, TILES)
-            o_sb = work.tile([P, GROUP, DV], F32, name="o_sb")
-            if j % 4 == 3:
+            c, r = divmod(j * GROUP, QUAD)
+            inv_sum = quads[c]["inv_sum"]
+            if members.start == 0:
+                grouped[j]["o_sb"] = work.tile([P, GROUP, DV], F32, name="o_sb")
+            o_sb = grouped[j]["o_sb"]
+            count = members.stop - members.start
+            if on_vector:
+                sums = inv_sum[:, r + members.start : r + members.stop]
                 nc.vector.tensor_tensor(
-                    out=o_sb[:], in0=grouped[j]["o_bank"][:],
-                    in1=grouped[j]["inv_sum"][:].unsqueeze(2).to_broadcast([P, GROUP, DV]), op=ALU.mult,
+                    out=o_sb[:, members, :], in0=grouped[j]["o_bank"][:, members, :],
+                    in1=sums.unsqueeze(2).to_broadcast([P, count, DV]), op=ALU.mult,
                 )
             else:
-                for m in range(GROUP):
+                for m in range(members.start, members.stop):
                     nc.scalar.activation(
                         out=o_sb[:, m, :], in_=grouped[j]["o_bank"][:, m, :], func=ACT.Copy,
-                        scale=grouped[j]["inv_sum"][:, m : m + 1],
+                        scale=inv_sum[:, r + m : r + m + 1],
                     )
+            rows = slice((i + members.start) * P, (i + members.stop) * P)
             nc.sync.dma_start(
-                out=out[b, i * P : (i + GROUP) * P, :].rearrange("(m p) w -> p m w", p=P), in_=o_sb[:]
+                out=out[b, rows, :].rearrange("(m p) w -> p m w", p=P), in_=o_sb[:, members, :]
             )
 
         load_keys(0)
@@ -426,8 +446,11 @@ def tile_dualmodehead_t_kernel(tc, q, k, v, mask, mode, out):
         turn_keys(0, 1)
         keep_keys(0, 1, nc.vector.tensor_copy)
         convert_mask(1)
-        gate(mask_bias[:, 1, 0:1])
+        convert_mask(2)
         blend_scale(1)
+        blend_add(1)
+        blend_hi(1)
+        blend_lo(1)
         scores(0)
         scores(1)
         add_mask(0)
@@ -436,9 +459,15 @@ def tile_dualmodehead_t_kernel(tc, q, k, v, mask, mode, out):
             if 0 <= n < N_TILES:
                 stage(n)
 
-        def on_group(stage, last):
+        def on_group(stage, last, *how):
             if 0 <= last < N_TILES and last % GROUP == GROUP - 1:
-                stage(last // GROUP)
+                stage(last // GROUP, *how)
+
+        def on_quad(stage, last):
+            if 0 <= last < N_TILES and last % QUAD == QUAD - 1:
+                stage(last // QUAD)
+
+        whole = slice(0, GROUP)
 
         for t in range(N_TILES + 6):
             b, i = divmod(t, TILES)
@@ -448,64 +477,65 @@ def tile_dualmodehead_t_kernel(tc, q, k, v, mask, mode, out):
                 load_values(b + 2)
             if t + 6 < TILES:
                 load_mask(t + 6)
-            on_group(product, t - 5)
+            if t < N_TILES:
+                on_group(product, t - 5, whole)
             on(exponent, t - 1)
             on(scores, t + 2)
-            on(regroup, t - 3)
-            on(turn, t - 2)
+            if t < N_TILES:
+                on(regroup, t - 3)
+                on(turn, t - 2)
             on(fold, t)
             on(add_mask, t + 1)
             on(row_max, t)
-            on_group(quantise, t - 4)
+            if t >= N_TILES:
+                on(regroup, t - 3)
+                on(turn, t - 2)
+                on_group(product, t - 5, whole)
+            on_group(quantise, t - 4, whole)
             if t == 5:
                 quantise_values(0)
             if b + 1 < B and i == 7:
                 quantise_values(b + 1)
-            if t == 0:
-                convert_mask(2)
-            if 0 <= t < 5:
+            if t == 2:
+                convert_mask(4)
+            if t in (0, 2, 3, 4):
                 convert_mask(t + 3)
-            on_group(finish, t - 5)
-            on_group(add_half_sums, t - 1)
-            if t == 0:
-                gate(mask_bias[:, t + 3, 0:1])
-                blend_add(1)
-            if t == 1:
-                gate(mask_bias[:, t + 3, 0:1])
-                group_quarter(0, 0)
-                blend_hi(1)
+            on_group(finish, t - 5, whole, (t - 5) // GROUP % 4 == 3)
+            on_quad(add_half_sums, t - 1)
             if t == 2:
                 gate(mask_bias[:, t + 3, 0:1])
-                blend_lo(1)
+                for quarter in (0, 1, 2):
+                    group_quarter(0, quarter)
             if t == 3:
                 gate(mask_bias[:, t + 3, 0:1])
-                for quarter in (1, 2, 3):
-                    group_quarter(0, quarter)
+                group_quarter(0, 3)
+                for quarter in (0, 1):
+                    group_quarter(1, quarter)
             if t == 4:
                 gate(mask_bias[:, t + 3, 0:1])
-                for quarter in range(4):
+                for quarter in (2, 3):
                     group_quarter(1, quarter)
             if t >= 5 and t % 2 == 1 and t < 8 * B - 14:
                 gate(grouped[(t - 4) // GROUP]["codes"][:, 0, 0, 0:1])
-                if t < TILES:
+                if t < 9:
                     prepare(2, (t - 5) // 2)
                 elif t == 9:
                     prepare(2, 2)
                     prepare(2, 3)
                 else:
                     prepare(3 + (t - 11) // TILES, (t - 11) % TILES // 2)
-            on_group(invert_sums, t - 4)
+            on_quad(invert_sums, t - 2)
             if b + 1 < B:
-                if i == 2:
+                if i == 1:
                     keep_queries(b + 1)
                 if i == 4:
                     keep_keys(b + 1, 0, nc.scalar.copy)
                 if i == 5:
                     keep_keys(b + 1, 1, nc.scalar.copy)
-            if t in (1, 3, 6, 7, 8):
+            if t - 1 in MASK_STEPS:
                 keep_mask(MASK_STEPS.index(t - 1))
             if b + 1 < B:
-                if i == 1:
+                if i == 0:
                     turn_queries(b + 1)
                 if i == 3:
                     turn_keys(b + 1, 0)

@@ -32,7 +32,8 @@ MASKS_ON_SCALAR = 4
 QUAD = 4
 GROUP = 2
 MASK_WORDS = 2
-MASKED = -(2.0**100)
+MASKED = 2.0**100
+HIGHEST = 2.0**127
 
 FLOPS = 2 * (2 * B * T * T * D) + 2 * B * T * T * DV
 
@@ -67,9 +68,9 @@ def tile_dualmodehead_t_kernel(tc, q, k, v, mask, mode, out):
         alpha = const.tile([P, 1], F32)
         nc.vector.reciprocal(out=alpha[:], in_=denom[:])
         c_meson = const.tile([P, 1], F32)
-        nc.vector.tensor_scalar_mul(out=c_meson[:], in0=alpha[:], scalar1=-(D**-0.5))
+        nc.vector.tensor_scalar_mul(out=c_meson[:], in0=alpha[:], scalar1=D**-0.5)
         c_baryon = const.tile([P, 1], F32)
-        nc.vector.tensor_scalar_add(out=c_baryon[:], in0=c_meson[:], scalar1=D**-0.5)
+        nc.vector.tensor_scalar_add(out=c_baryon[:], in0=c_meson[:], scalar1=-(D**-0.5))
 
         mask_bias = const.tile([P, TILES, T], BF16)
 
@@ -301,19 +302,18 @@ def tile_dualmodehead_t_kernel(tc, q, k, v, mask, mode, out):
                 )
             live[n]["s_masked"] = s_masked
 
-        def fold(n):
-            if mask_on_tensor(n, 1):
-                folded = work.tile([P, BANK], F32, name="folded", bufs=2)
-                nc.vector.tensor_tensor(
-                    out=folded[:], in0=live[n]["s"][1][:], in1=live[n]["s_masked"][:, 0:BANK], op=ALU.max
+        def row_min(n):
+            if on_tensor(n):
+                lowest = work.tile([P, BANK], F32, name="lowest")
+                nc.vector.tensor_tensor_scan(
+                    out=lowest[:], data0=live[n]["s"][1][:], data1=live[n]["s_masked"][:, 0:BANK], initial=HIGHEST,
+                    op0=ALU.min, op1=ALU.min,
                 )
-                live[n]["folded"] = folded
-
-        def row_max(n):
-            neg_max = small.tile([P, 1], F32, name="neg_max")
-            source = live[n]["folded"] if mask_on_tensor(n, 1) else live[n]["s_masked"]
-            nc.vector.tensor_reduce(out=neg_max[:], in_=source[:], axis=AX.X, op=ALU.max, negate=True)
-            live[n]["neg_max"] = neg_max
+                live[n]["neg_max"] = lowest[:, BANK - 1 : BANK]
+            else:
+                neg_max = small.tile([P, 1], F32, name="neg_max")
+                nc.vector.tensor_reduce(out=neg_max[:], in_=live[n]["s_masked"][:], axis=AX.X, op=ALU.min)
+                live[n]["neg_max"] = neg_max[:, 0:1]
 
         def exponent(n):
             j, m = divmod(n, GROUP)
@@ -326,20 +326,20 @@ def tile_dualmodehead_t_kernel(tc, q, k, v, mask, mode, out):
                     quads[c]["half_sums"] = small.tile([P, QUAD, HALVES], F32, name="half_sums")
             e = work.tile([P, T], BF16, name="e")
             row_sum = quads[c]["row_sum"][:, r : r + 1]
-            neg_max = live[n]["neg_max"][:, 0:1]
+            neg_max = live[n]["neg_max"]
             if mask_on_tensor(n, 1):
                 half_sums = quads[c]["half_sums"]
                 nc.scalar.activation(
-                    out=e[:, BANK:T], in_=live[n]["s"][1][:], func=ACT.Exp, bias=neg_max, scale=1.0,
+                    out=e[:, BANK:T], in_=live[n]["s"][1][:], func=ACT.Exp, bias=neg_max, scale=-1.0,
                     accum_out=half_sums[:, r, 1:2],
                 )
                 nc.scalar.activation(
-                    out=e[:, 0:BANK], in_=live[n]["s_masked"][:, 0:BANK], func=ACT.Exp, bias=neg_max, scale=1.0,
+                    out=e[:, 0:BANK], in_=live[n]["s_masked"][:, 0:BANK], func=ACT.Exp, bias=neg_max, scale=-1.0,
                     accum_out=half_sums[:, r, 0:1],
                 )
             else:
                 nc.scalar.activation(
-                    out=e[:], in_=live[n]["s_masked"][:], func=ACT.Exp, bias=neg_max, scale=1.0, accum_out=row_sum
+                    out=e[:], in_=live[n]["s_masked"][:], func=ACT.Exp, bias=neg_max, scale=-1.0, accum_out=row_sum
                 )
             live[n]["e"] = e
 
@@ -386,12 +386,12 @@ def tile_dualmodehead_t_kernel(tc, q, k, v, mask, mode, out):
 
         def product(j, members):
             ops = operand[(j * GROUP) // TILES]
-            if members.start == 0:
-                grouped[j]["o_bank"] = psum_t.tile([P, GROUP, DV], F32, name="o_bank", tag="bank_t")
+            o_bank = psum_t.tile([P, GROUP, DV], F32, name="o_bank", tag="bank_t")
+            grouped[j]["o_bank", members.start] = o_bank
             for m in range(members.start, members.stop):
                 for g in range(PASSES):
                     nc.tensor.matmul_mx(
-                        out=grouped[j]["o_bank"][:, m, :],
+                        out=o_bank[:, m, :],
                         lhsT=grouped[j]["codes"][:, m, g, :].bitcast(FP8X4),
                         lhsT_scale=grouped[j]["scales"][:, m, g, :],
                         rhs=ops["v_codes"][:, g * DV : (g + 1) * DV].bitcast(FP8X4),
@@ -404,20 +404,19 @@ def tile_dualmodehead_t_kernel(tc, q, k, v, mask, mode, out):
             b, i = divmod(j * GROUP, TILES)
             c, r = divmod(j * GROUP, QUAD)
             inv_sum = quads[c]["inv_sum"]
-            if members.start == 0:
-                grouped[j]["o_sb"] = work.tile([P, GROUP, DV], F32, name="o_sb")
-            o_sb = grouped[j]["o_sb"]
+            o_bank = grouped[j]["o_bank", members.start]
+            o_sb = work.tile([P, GROUP, DV], F32, name="o_sb")
             count = members.stop - members.start
             if on_vector:
                 sums = inv_sum[:, r + members.start : r + members.stop]
                 nc.vector.tensor_tensor(
-                    out=o_sb[:, members, :], in0=grouped[j]["o_bank"][:, members, :],
+                    out=o_sb[:, members, :], in0=o_bank[:, members, :],
                     in1=sums.unsqueeze(2).to_broadcast([P, count, DV]), op=ALU.mult,
                 )
             else:
                 for m in range(members.start, members.stop):
                     nc.scalar.activation(
-                        out=o_sb[:, m, :], in_=grouped[j]["o_bank"][:, m, :], func=ACT.Copy,
+                        out=o_sb[:, m, :], in_=o_bank[:, m, :], func=ACT.Copy,
                         scale=inv_sum[:, r + m : r + m + 1],
                     )
             rows = slice((i + members.start) * P, (i + members.stop) * P)
@@ -460,7 +459,7 @@ def tile_dualmodehead_t_kernel(tc, q, k, v, mask, mode, out):
                 stage(n)
 
         def on_group(stage, last, *how):
-            if 0 <= last < N_TILES and last % GROUP == GROUP - 1:
+            if 0 <= last < N_TILES - GROUP and last % GROUP == GROUP - 1:
                 stage(last // GROUP, *how)
 
         def on_quad(stage, last):
@@ -468,8 +467,10 @@ def tile_dualmodehead_t_kernel(tc, q, k, v, mask, mode, out):
                 stage(last // QUAD)
 
         whole = slice(0, GROUP)
+        first, second = slice(0, 1), slice(1, GROUP)
+        last_group = N_TILES // GROUP - 1
 
-        for t in range(N_TILES + 6):
+        for t in range(N_TILES + 4):
             b, i = divmod(t, TILES)
             if i == (3 if b == 0 else 0) and b + 2 < B:
                 load_keys(b + 2)
@@ -484,14 +485,20 @@ def tile_dualmodehead_t_kernel(tc, q, k, v, mask, mode, out):
             if t < N_TILES:
                 on(regroup, t - 3)
                 on(turn, t - 2)
-            on(fold, t)
             on(add_mask, t + 1)
-            on(row_max, t)
+            on(row_min, t)
+            if t == N_TILES + 2:
+                quantise(last_group, first)
             if t >= N_TILES:
                 on(regroup, t - 3)
                 on(turn, t - 2)
                 on_group(product, t - 5, whole)
             on_group(quantise, t - 4, whole)
+            if t == N_TILES + 2:
+                product(last_group, first)
+            if t == N_TILES + 3:
+                quantise(last_group, second)
+                product(last_group, second)
             if t == 5:
                 quantise_values(0)
             if b + 1 < B and i == 7:
@@ -501,6 +508,9 @@ def tile_dualmodehead_t_kernel(tc, q, k, v, mask, mode, out):
             if t in (0, 2, 3, 4):
                 convert_mask(t + 3)
             on_group(finish, t - 5, whole, (t - 5) // GROUP % 4 == 3)
+            if t == N_TILES + 3:
+                finish(last_group, first, False)
+                finish(last_group, second, True)
             on_quad(add_half_sums, t - 1)
             if t == 2:
                 gate(mask_bias[:, t + 3, 0:1])

from contextlib import ExitStack

import concourse.mybir as mybir
from concourse.masks import make_identity

F32 = mybir.dt.float32
BF16 = mybir.dt.bfloat16
I32 = mybir.dt.int32
U32 = mybir.dt.uint32
U8 = mybir.dt.uint8
FP8X4 = mybir.dt.float8_e4m3fn_x4
ALU = mybir.AluOpType
ACT = mybir.ActivationFunctionType
AX = mybir.AxisListType

B, T, D, DV = 8, 1024, 128, 256
P = 128
TILES = T // P
N_TILES = B * TILES
BANK = 512
HALVES = T // BANK
BLOCKS = BANK // P
PACK = 4
K_PASS = P * PACK
PASSES = T // K_PASS
VECTOR_REGROUPS_FROM = N_TILES - 3
VECTOR_FINISHES_FROM = N_TILES - 2
FIRST_ON_TENSOR = 5
MASK_STEPS = (0, 2, 5, 6, 7)
TURNED = 5
MASKS_ON_SCALAR = 4
QUAD = 4
GROUP = 2
MASK_WORDS = 2
MASKED = 2.0**100
HIGHEST = 2.0**127

FLOPS = 2 * (2 * B * T * T * D) + 2 * B * T * T * DV


def tile_dualmodehead_t_kernel(tc, q, k, v, mask, mode, out):
    nc = tc.nc
    mask_rows = mask.bitcast(I32).rearrange("o q w -> (o q) w")
    assert mask_rows.shape[1] == T * MASK_WORDS

    with ExitStack() as ctx:
        const = ctx.enter_context(tc.tile_pool(name="const", bufs=1))
        loads = ctx.enter_context(tc.tile_pool(name="loads", bufs=2))
        batch = ctx.enter_context(tc.tile_pool(name="batch", bufs=2))
        work = ctx.enter_context(tc.tile_pool(name="work", bufs=4))
        small = ctx.enter_context(tc.tile_pool(name="small", bufs=8))
        psum_a = ctx.enter_context(tc.psum_pool(name="psum_a", bufs=2))
        psum_b = ctx.enter_context(tc.psum_pool(name="psum_b", bufs=3))
        psum_t = ctx.enter_context(tc.psum_pool(name="psum_t", bufs=3))
        ctx.enter_context(tc.manual_schedule())

        ident_bf = const.tile([P, P], BF16)
        make_identity(nc, ident_bf[:])
        ident_f32 = const.tile([P, P], F32)
        make_identity(nc, ident_f32[:])

        mode_bc = const.tile([P, 1], BF16)
        nc.sync.dma_start(out=mode_bc[:], in_=mode.partition_broadcast(P))
        exp_neg = const.tile([P, 1], F32)
        nc.scalar.activation(out=exp_neg[:], in_=mode_bc[:], func=ACT.Exp, scale=-1.0)
        denom = const.tile([P, 1], F32)
        nc.vector.tensor_scalar_add(out=denom[:], in0=exp_neg[:], scalar1=1.0)
        alpha = const.tile([P, 1], F32)
        nc.vector.reciprocal(out=alpha[:], in_=denom[:])
        c_meson = const.tile([P, 1], F32)
        nc.vector.tensor_scalar_mul(out=c_meson[:], in0=alpha[:], scalar1=D**-0.5)
        c_baryon = const.tile([P, 1], F32)
        nc.vector.tensor_scalar_add(out=c_baryon[:], in0=c_meson[:], scalar1=-(D**-0.5))

        mask_bias = const.tile([P, TILES, T], BF16)

        mask_turned = const.tile([P, TURNED, BLOCKS, P], F32)

        mask_raw = {}

        def load_mask(i):
            mask_raw[i] = loads.tile([P, T, MASK_WORDS], I32, name="mask_raw", bufs=6)
            nc.sync.dma_start(
                out=mask_raw[i][:].rearrange("p k w -> p (k w)"), in_=mask_rows[i * P : (i + 1) * P, :]
            )

        def convert_mask(i):
            if i < MASKS_ON_SCALAR:
                nc.scalar.activation(
                    out=mask_bias[:, i, :], in_=mask_raw[i][:].bitcast(U32)[:, :, 0], func=ACT.Copy,
                    scale=-MASKED, bias=MASKED,
                )
                return
            nc.vector.tensor_scalar(
                out=mask_bias[:, i, :], in0=mask_raw[i][:, :, 0], scalar1=-MASKED, scalar2=MASKED, op0=ALU.mult, op1=ALU.add
            )

        mask_banks = {}

        def turn_mask(i, pool, tag):
            bank = pool.tile([P, BLOCKS, P], BF16, name="bank_m", tag=tag)
            for r in range(BLOCKS):
                nc.tensor.transpose(bank[:, r, :], mask_bias[:, i, BANK + r * P : BANK + (r + 1) * P], ident_bf[:])
            mask_banks[i] = bank

        def keep_mask(i):
            nc.scalar.activation(
                out=mask_turned[:, i, :, :], in_=mask_banks[i][:], func=ACT.Copy, scale=1.0
            )

        natural = {}
        operand = {}

        def load_keys(b):
            k_nat = loads.tile([P, TILES, D], BF16, name="k_nat")
            nc.sync.dma_start(out=k_nat[:], in_=k[b].rearrange("(j p) d -> p j d", p=P))
            natural[b] = {"k": k_nat}
            operand[b] = {}

        def load_queries(b):
            q_nat = loads.tile([P, TILES, D], BF16, name="q_nat")
            nc.sync.dma_start(out=q_nat[:], in_=q[b].rearrange("(j p) d -> p j d", p=P))
            natural[b]["q"] = q_nat

        def load_values(b):
            v_raw = loads.tile([P, PASSES, PACK, DV], BF16, name="v_raw", bufs=3)
            nc.sync.dma_start(
                out=v_raw[:].rearrange("p g (u e) w -> p (g u) (e w)", e=2),
                in_=v[b].rearrange("(c p e) w -> p c (e w)", p=P, e=2),
            )
            natural[b]["v"] = v_raw

        def gate(column):
            passed = small.tile([P, 1], column.dtype, name="passed")
            nc.gpsimd.tensor_copy(out=passed[:], in_=column)

        def blend_scale(b):
            k_nat = natural[b]["k"]
            k_meson = loads.tile([P, TILES, D], F32, name="k_meson")
            k_baryon = loads.tile([P, TILES, D], F32, name="k_baryon")
            natural[b]["k_meson"] = k_meson
            natural[b]["k_baryon"] = k_baryon
            nc.gpsimd.tensor_scalar(
                out=k_meson[:], in0=k_nat[:], scalar1=c_meson[:, 0:1], scalar2=0.0, op0=ALU.mult, op1=ALU.add
            )
            nc.gpsimd.tensor_scalar(
                out=k_baryon[:, :, 1:D], in0=k_nat[:, :, 0 : D - 1], scalar1=c_baryon[:, 0:1], scalar2=0.0,
                op0=ALU.mult, op1=ALU.add,
            )
            nc.gpsimd.tensor_scalar(
                out=k_baryon[:, :, 0:1], in0=k_nat[:, :, D - 1 : D], scalar1=c_baryon[:, 0:1], scalar2=0.0,
                op0=ALU.mult, op1=ALU.add,
            )

        def blend_add(b):
            k_meson = natural[b]["k_meson"]
            nc.gpsimd.tensor_tensor(out=k_meson[:], in0=k_meson[:], in1=natural[b]["k_baryon"][:], op=ALU.add)

        def blend_hi(b):
            k_parts = loads.tile([P, 2, TILES, D], BF16, name="k_parts")
            natural[b]["k_parts"] = k_parts
            nc.gpsimd.tensor_scalar(
                out=k_parts[:, 0, :, :], in0=natural[b]["k_meson"][:], scalar1=1.0, scalar2=0.0,
                op0=ALU.mult, op1=ALU.add,
            )

        def blend_lo(b):
            k_parts = natural[b]["k_parts"]
            nc.gpsimd.tensor_tensor(
                out=k_parts[:, 1, :, :], in0=natural[b]["k_meson"][:], in1=k_parts[:, 0, :, :], op=ALU.subtract
            )

        def group_quarter(b, quarter):
            if quarter == 0:
                natural[b]["v_grouped"] = loads.tile(
                    [P, PASSES, DV, PACK], BF16, name="v_grouped", align_bytes=64, bufs=3
                )
            g, half = divmod(quarter, 2)
            columns = slice(half * (DV // 2), (half + 1) * (DV // 2))
            nc.gpsimd.tensor_scalar(
                out=natural[b]["v_grouped"][:, g, columns, :],
                in0=natural[b]["v"][:, g, :, columns].rearrange("p t w -> p w t"),
                scalar1=1.0, scalar2=0.0, op0=ALU.mult, op1=ALU.add,
            )

        def prepare(b, piece):
            group_quarter(b, piece)
            if piece == 0:
                blend_scale(b)
            elif piece == 1:
                blend_add(b)
            elif piece == 2:
                blend_hi(b)
            else:
                blend_lo(b)

        def blend_first_keys():
            k_nat = natural[0]["k"]
            k_meson = loads.tile([P, TILES, D], F32, name="k_meson")
            k_baryon = loads.tile([P, TILES, D], F32, name="k_baryon")
            k_parts = loads.tile([P, 2, TILES, D], BF16, name="k_parts")
            natural[0]["k_parts"] = k_parts
            halves = [slice(h * BLOCKS, (h + 1) * BLOCKS) for h in range(HALVES)]
            for js in halves:
                nc.vector.tensor_scalar_mul(out=k_meson[:, js, :], in0=k_nat[:, js, :], scalar1=c_meson[:, 0:1])
            for js in halves:
                nc.vector.scalar_tensor_tensor(
                    out=k_baryon[:, js, 1:D], in0=k_nat[:, js, 0 : D - 1], scalar=c_baryon[:, 0:1],
                    in1=k_meson[:, js, 1:D], op0=ALU.mult, op1=ALU.add,
                )
                nc.vector.scalar_tensor_tensor(
                    out=k_baryon[:, js, 0:1], in0=k_nat[:, js, D - 1 : D], scalar=c_baryon[:, 0:1],
                    in1=k_meson[:, js, 0:1], op0=ALU.mult, op1=ALU.add,
                )
            for js in halves:
                nc.vector.tensor_copy(out=k_parts[:, 0, js, :], in_=k_baryon[:, js, :])
            for js in halves:
                nc.vector.tensor_tensor(
                    out=k_parts[:, 1, js, :], in0=k_baryon[:, js, :], in1=k_parts[:, 0, js, :], op=ALU.subtract
                )

        def turn_queries(b):
            bank = psum_t.tile([P, T], BF16, name="bank_q", tag="bank_t")
            for j in range(TILES):
                nc.tensor.transpose(bank[:, j * P : (j + 1) * P], natural[b]["q"][:, j, :], ident_bf[:])
            operand[b]["bank_q"] = bank

        def keep_queries(b):
            qT = batch.tile([P, T], BF16, name="qT")
            nc.scalar.copy(out=qT[:], in_=operand[b]["bank_q"][:])
            operand[b]["qT"] = qT

        def turn_keys(b, h):
            if h == 0:
                operand[b]["kT"] = batch.tile([P, HALVES, 2, BANK], BF16, name="kT")
            bank = psum_t.tile([P, 2, BLOCKS, P], BF16, name="bank_k", tag="bank_t")
            for part in range(2):
                for r in range(BLOCKS):
                    nc.tensor.transpose(
                        bank[:, part, r, :], natural[b]["k_parts"][:, part, h * BLOCKS + r, :], ident_bf[:]
                    )
            operand[b]["bank_k"] = bank

        def keep_keys(b, h, copy):
            copy(
                out=operand[b]["kT"][:, h, :, :], in_=operand[b]["bank_k"][:].rearrange("p a r c -> p a (r c)")
            )

        def quantise_values(b):
            v_codes = batch.tile([P, PASSES * DV], U32, name="v_codes", align_bytes=64)
            v_scales = batch.tile([P, PASSES * DV], U8, name="v_scales", align_bytes=64)
            nc.vector.quantize_mx(
                out=v_codes[:].bitcast(FP8X4),
                scales=v_scales[:],
                in_=natural[b]["v_grouped"][:].rearrange("p g w t -> p (g w t)"),
            )
            operand[b]["v_codes"] = v_codes
            operand[b]["v_scales"] = v_scales

        live = {}
        quads = {}
        grouped = {}

        def on_tensor(n):
            return n >= FIRST_ON_TENSOR

        def mask_on_tensor(n, h):
            return h == HALVES - 1 and on_tensor(n)

        def scores(n):
            b, i = divmod(n, TILES)
            qT_tile = operand[b]["qT"][:, i * P : (i + 1) * P]
            live[n] = {"s": []}
            for h in range(HALVES):
                s_bank = (psum_a, psum_b)[h].tile([P, BANK], F32, name="s_bank", tag="s_bank")
                nc.tensor.matmul(s_bank[:], lhsT=qT_tile, rhs=operand[b]["kT"][:, h, 0, :], start=True, stop=False)
                nc.tensor.matmul(
                    s_bank[:], lhsT=qT_tile, rhs=operand[b]["kT"][:, h, 1, :], start=False,
                    stop=not mask_on_tensor(n, h),
                )
                if mask_on_tensor(n, h) and (b == 0 or i >= TURNED):
                    nc.tensor.matmul(
                        s_bank[:], lhsT=ident_bf[:], rhs=mask_bias[:, i, BANK:T], start=False, stop=True
                    )
                elif mask_on_tensor(n, h):
                    for r in range(BLOCKS):
                        nc.tensor.matmul(
                            s_bank[:, r * P : (r + 1) * P], lhsT=mask_turned[:, i, r, :], rhs=ident_f32[:],
                            start=False, stop=(r == BLOCKS - 1), is_transpose=True,
                        )
                live[n]["s"].append(s_bank)

        def add_mask(n):
            i = n % TILES
            s_masked = work.tile([P, T], F32, name="s_masked")
            for h in range(HALVES):
                if mask_on_tensor(n, h):
                    continue
                keys = slice(h * BANK, (h + 1) * BANK)
                nc.vector.tensor_tensor(
                    out=s_masked[:, keys], in0=live[n]["s"][h][:], in1=mask_bias[:, i, keys], op=ALU.add
                )
            live[n]["s_masked"] = s_masked

        def row_min(n):
            if on_tensor(n):
                lowest = work.tile([P, BANK], F32, name="lowest")
                nc.vector.tensor_tensor_scan(
                    out=lowest[:], data0=live[n]["s"][1][:], data1=live[n]["s_masked"][:, 0:BANK], initial=HIGHEST,
                    op0=ALU.min, op1=ALU.min,
                )
                live[n]["neg_max"] = lowest[:, BANK - 1 : BANK]
            else:
                neg_max = small.tile([P, 1], F32, name="neg_max")
                nc.vector.tensor_reduce(out=neg_max[:], in_=live[n]["s_masked"][:], axis=AX.X, op=ALU.min)
                live[n]["neg_max"] = neg_max[:, 0:1]

        def exponent(n):
            j, m = divmod(n, GROUP)
            if m == 0:
                grouped[j] = {}
            c, r = divmod(n, QUAD)
            if r == 0:
                quads[c] = {"row_sum": small.tile([P, QUAD], F32, name="row_sum")}
                if on_tensor(n + QUAD - 1):
                    quads[c]["half_sums"] = small.tile([P, QUAD, HALVES], F32, name="half_sums")
            e = work.tile([P, T], BF16, name="e")
            row_sum = quads[c]["row_sum"][:, r : r + 1]
            neg_max = live[n]["neg_max"]
            if mask_on_tensor(n, 1):
                half_sums = quads[c]["half_sums"]
                nc.scalar.activation(
                    out=e[:, BANK:T], in_=live[n]["s"][1][:], func=ACT.Exp, bias=neg_max, scale=-1.0,
                    accum_out=half_sums[:, r, 1:2],
                )
                nc.scalar.activation(
                    out=e[:, 0:BANK], in_=live[n]["s_masked"][:, 0:BANK], func=ACT.Exp, bias=neg_max, scale=-1.0,
                    accum_out=half_sums[:, r, 0:1],
                )
            else:
                nc.scalar.activation(
                    out=e[:], in_=live[n]["s_masked"][:], func=ACT.Exp, bias=neg_max, scale=-1.0, accum_out=row_sum
                )
            live[n]["e"] = e

        def add_half_sums(c):
            halved = [r for r in range(QUAD) if on_tensor(c * QUAD + r)]
            if halved:
                half_sums = quads[c]["half_sums"]
                rs = slice(halved[0], QUAD)
                nc.gpsimd.tensor_tensor(
                    out=quads[c]["row_sum"][:, rs], in0=half_sums[:, rs, 0], in1=half_sums[:, rs, 1], op=ALU.add
                )

        def invert_sums(c):
            inv_sum = small.tile([P, QUAD], F32, name="inv_sum")
            nc.vector.reciprocal(out=inv_sum[:], in_=quads[c]["row_sum"][:])
            quads[c]["inv_sum"] = inv_sum

        def turn(n):
            e_words = live[n]["e"][:].bitcast(F32)
            eT_bank = psum_t.tile([P, PASSES * 2, P], F32, name="eT_bank", tag="bank_t")
            for c in range(PASSES * 2):
                nc.tensor.transpose(eT_bank[:, c, :], e_words[:, c * P : (c + 1) * P], ident_f32[:])
            live[n]["eT_bank"] = eT_bank

        def regroup(n):
            j, m = divmod(n, GROUP)
            if m == 0:
                grouped[j]["e"] = work.tile([P, GROUP, PASSES * P * PACK], BF16, name="e_grouped", align_bytes=64)
            copy = nc.vector.tensor_copy if n >= VECTOR_REGROUPS_FROM else nc.scalar.copy
            copy(
                out=grouped[j]["e"][:, m, :].bitcast(F32).rearrange("p (g q u) -> p g q u", g=PASSES, u=2),
                in_=live[n]["eT_bank"][:].rearrange("p (g u) q -> p g q u", u=2),
            )

        def quantise(j, members):
            if members.start == 0:
                grouped[j]["codes"] = work.tile([P, GROUP, PASSES, P], U32, name="e_codes", align_bytes=64)
                grouped[j]["scales"] = work.tile([P, GROUP, PASSES, P], U8, name="e_scales", align_bytes=64)
            nc.vector.quantize_mx(
                out=grouped[j]["codes"][:, members, :, :].rearrange("p m g q -> p (m g q)").bitcast(FP8X4),
                scales=grouped[j]["scales"][:, members, :, :].rearrange("p m g q -> p (m g q)"),
                in_=grouped[j]["e"][:, members, :].rearrange("p m c -> p (m c)"),
            )

        def product(j, members):
            ops = operand[(j * GROUP) // TILES]
            o_bank = psum_t.tile([P, GROUP, DV], F32, name="o_bank", tag="bank_t")
            grouped[j]["o_bank", members.start] = o_bank
            for m in range(members.start, members.stop):
                for g in range(PASSES):
                    nc.tensor.matmul_mx(
                        out=o_bank[:, m, :],
                        lhsT=grouped[j]["codes"][:, m, g, :].bitcast(FP8X4),
                        lhsT_scale=grouped[j]["scales"][:, m, g, :],
                        rhs=ops["v_codes"][:, g * DV : (g + 1) * DV].bitcast(FP8X4),
                        rhs_scale=ops["v_scales"][:, g * DV : (g + 1) * DV],
                        start=(g == 0),
                        stop=(g == PASSES - 1),
                    )

        def finish(j, members, on_vector):
            b, i = divmod(j * GROUP, TILES)
            c, r = divmod(j * GROUP, QUAD)
            inv_sum = quads[c]["inv_sum"]
            o_bank = grouped[j]["o_bank", members.start]
            o_sb = work.tile([P, GROUP, DV], F32, name="o_sb")
            count = members.stop - members.start
            if on_vector:
                sums = inv_sum[:, r + members.start : r + members.stop]
                nc.vector.tensor_tensor(
                    out=o_sb[:, members, :], in0=o_bank[:, members, :],
                    in1=sums.unsqueeze(2).to_broadcast([P, count, DV]), op=ALU.mult,
                )
            else:
                for m in range(members.start, members.stop):
                    nc.scalar.activation(
                        out=o_sb[:, m, :], in_=o_bank[:, m, :], func=ACT.Copy,
                        scale=inv_sum[:, r + m : r + m + 1],
                    )
            rows = slice((i + members.start) * P, (i + members.stop) * P)
            nc.sync.dma_start(
                out=out[b, rows, :].rearrange("(m p) w -> p m w", p=P), in_=o_sb[:, members, :]
            )

        load_keys(0)
        load_queries(0)
        load_mask(0)
        load_mask(1)
        load_keys(1)
        load_mask(2)
        load_queries(1)
        load_mask(3)
        load_values(0)
        load_mask(4)
        load_mask(5)
        load_values(1)
        blend_first_keys()
        turn_queries(0)
        keep_queries(0)
        turn_keys(0, 0)
        keep_keys(0, 0, nc.scalar.copy)
        convert_mask(0)
        turn_keys(0, 1)
        keep_keys(0, 1, nc.vector.tensor_copy)
        convert_mask(1)
        convert_mask(2)
        blend_scale(1)
        blend_add(1)
        blend_hi(1)
        blend_lo(1)
        scores(0)
        scores(1)
        add_mask(0)

        def on(stage, n):
            if 0 <= n < N_TILES:
                stage(n)

        def on_group(stage, last, *how):
            if 0 <= last < N_TILES - GROUP and last % GROUP == GROUP - 1:
                stage(last // GROUP, *how)

        def on_quad(stage, last):
            if 0 <= last < N_TILES and last % QUAD == QUAD - 1:
                stage(last // QUAD)

        whole = slice(0, GROUP)
        first, second = slice(0, 1), slice(1, GROUP)
        last_group = N_TILES // GROUP - 1

        for t in range(N_TILES + 4):
            b, i = divmod(t, TILES)
            if i == (3 if b == 0 else 0) and b + 2 < B:
                load_keys(b + 2)
                load_queries(b + 2)
                load_values(b + 2)
            if t + 6 < TILES:
                load_mask(t + 6)
            if t < N_TILES:
                on_group(product, t - 5, whole)
            on(exponent, t - 1)
            on(scores, t + 2)
            if t < N_TILES:
                on(regroup, t - 3)
                on(turn, t - 2)
            on(add_mask, t + 1)
            on(row_min, t)
            if t == N_TILES + 2:
                quantise(last_group, first)
            if t >= N_TILES:
                on(regroup, t - 3)
                on(turn, t - 2)
                on_group(product, t - 5, whole)
            on_group(quantise, t - 4, whole)
            if t == N_TILES + 2:
                product(last_group, first)
            if t == N_TILES + 3:
                quantise(last_group, second)
                product(last_group, second)
            if t == 5:
                quantise_values(0)
            if b + 1 < B and i == 7:
                quantise_values(b + 1)
            if t == 2:
                convert_mask(4)
            if t in (0, 2, 3, 4):
                convert_mask(t + 3)
            on_group(finish, t - 5, whole, (t - 5) // GROUP % 4 == 3)
            if t == N_TILES + 3:
                finish(last_group, first, False)
                finish(last_group, second, True)
            on_quad(add_half_sums, t - 1)
            if t == 2:
                gate(mask_bias[:, t + 3, 0:1])
                for quarter in (0, 1, 2):
                    group_quarter(0, quarter)
            if t == 3:
                gate(mask_bias[:, t + 3, 0:1])
                group_quarter(0, 3)
                for quarter in (0, 1):
                    group_quarter(1, quarter)
            if t == 4:
                gate(mask_bias[:, t + 3, 0:1])
                for quarter in (2, 3):
                    group_quarter(1, quarter)
            if t >= 5 and t % 2 == 1 and t < 8 * B - 14:
                gate(grouped[(t - 4) // GROUP]["codes"][:, 0, 0, 0:1])
                if t < 9:
                    prepare(2, (t - 5) // 2)
                elif t == 9:
                    prepare(2, 2)
                    prepare(2, 3)
                else:
                    prepare(3 + (t - 11) // TILES, (t - 11) % TILES // 2)
            on_quad(invert_sums, t - 2)
            if b + 1 < B:
                if i == 1:
                    keep_queries(b + 1)
                if i == 4:
                    keep_keys(b + 1, 0, nc.scalar.copy)
                if i == 5:
                    keep_keys(b + 1, 1, nc.scalar.copy)
            if t - 1 in MASK_STEPS:
                keep_mask(MASK_STEPS.index(t - 1))
            if b + 1 < B:
                if i == 0:
                    turn_queries(b + 1)
                if i == 3:
                    turn_keys(b + 1, 0)
                if i == 4:
                    turn_keys(b + 1, 1)
            if t in MASK_STEPS:
                turn_mask(MASK_STEPS.index(t), psum_t, "bank_t")
